import numpy as np
import ml_dtypes


def mxq(x, axis, fmt="e4m3"):
    dtype, down = {"e4m3": (ml_dtypes.float8_e4m3fn, 7), "e5m2": (ml_dtypes.float8_e5m2, 14)}[fmt]
    v = np.moveaxis(np.asarray(x, np.float32).astype(ml_dtypes.bfloat16).astype(np.float64), axis, -1)
    blocks = v.reshape(v.shape[:-1] + (-1, 32))
    amax = np.abs(blocks).max(-1, keepdims=True)
    byte = np.maximum(np.where(amax > 0, np.frexp(amax)[1] - 1 + 127, 0) - down, 1)
    scale = np.exp2(byte - 127.0)
    codes = (blocks / scale).astype(np.float32).astype(dtype).astype(np.float64)
    return np.moveaxis((codes * scale).reshape(v.shape), -1, axis)


WIDE = False


def mx_kscale(k):
    if not WIDE:
        return np.ones(k)
    levels = np.array([10, -10, 5, -5, 0])
    if k % 512:
        return np.exp2(np.random.permutation(np.resize(levels, k // 32))).repeat(32)
    a = np.empty((k // 512, 16))
    for p in range(k // 512):
        a[p, :8] = np.random.permutation(np.resize(levels, 8))
        for g in range(8):
            far = levels[np.abs(levels - a[p, g]) >= 10]
            a[p, g + 8] = far[np.random.randint(len(far))]
    return np.exp2(a.ravel()).repeat(32)


BF16 = ml_dtypes.bfloat16


def bf(x):
    return np.asarray(x, np.float32).astype(BF16)


def f64(x):
    return np.asarray(x).astype(np.float64)


B, T, C, F = 4, 512, 512, 2048
M = T


def silu(v):
    return v / (1.0 + np.exp(-v))


def sigmoid(v):
    return 1.0 / (1.0 + np.exp(-v))


def setup_inputs():
    t = mx_kscale(F)
    x = np.random.standard_normal((B, T, C)) + 0.5 * np.random.standard_normal((B, 1, C))
    return {"h": bf(silu(np.random.standard_normal((B, T, F)) * 0.85) * t),
            "x": bf(x),
            "memory": bf(np.random.standard_normal((1, M, C)) * 6.0 / np.sqrt(C)),
            "w2": bf(np.random.standard_normal((F, C)) * 3.0 / np.sqrt(F) / t[:, None]),
            "b2": bf(np.random.standard_normal(C) * 0.5)}


def core(h, x, memory, w2, b2):
    update_gate = sigmoid((mxq(f64(h), 2, "e4m3") @ mxq(f64(w2), 0, "e4m3")) + f64(b2))
    x_mean = f64(x).mean(axis=1, keepdims=True)
    new_mem = f64(memory) * (1.0 - update_gate) + x_mean * update_gate
    return new_mem.mean(axis=0, keepdims=True)


def e4m3fn_bytes(y):
    return np.clip(np.asarray(y, np.float64), -448.0, 448.0).astype(np.float32).astype(ml_dtypes.float8_e4m3fn).view(np.uint8)


def reference(h, x, memory, w2, b2):
    out = core(h, x, memory, w2, b2)
    s = np.max(np.abs(out), axis=-1, keepdims=True) / 448.0
    return out, e4m3fn_bytes(out / s)

@@ -1,0 +1,422 @@
+from contextlib import ExitStack
+
+import concourse.mybir as mybir
+from concourse.masks import make_identity
+
+F32 = mybir.dt.float32
+BF16 = mybir.dt.bfloat16
+U32 = mybir.dt.uint32
+U8 = mybir.dt.uint8
+FP8X4 = mybir.dt.float8_e4m3fn_x4
+FP8 = mybir.dt.float8_e4m3fn
+ALU = mybir.AluOpType
+ACT = mybir.ActivationFunctionType
+AX = mybir.AxisListType
+
+NB, T, C, F = 4, 512, 512, 2048
+P = 128
+NMT = T // P
+NCT = C // P
+NG = F // 512
+FLOPS = 2 * NB * T * F * C
+
+XN = 64
+W_SPLIT = 320
+
+
+def tile_dynamicmemorybank_pb_kernel(tc, h, x, memory, w2, b2, out_0, out_1):
+    nc = tc.nc
+    with ExitStack() as ctx:
+        consts = ctx.enter_context(tc.tile_pool(name="consts", bufs=1))
+        loads = ctx.enter_context(tc.tile_pool(name="loads", bufs=16))
+        wstage = ctx.enter_context(tc.tile_pool(name="wstage", bufs=2))
+        hstage = ctx.enter_context(tc.tile_pool(name="hstage", bufs=2))
+        epil = ctx.enter_context(tc.tile_pool(name="epil", bufs=2))
+        psum_t = ctx.enter_context(tc.psum_pool(name="psum_t", bufs=4))
+        psum_a = ctx.enter_context(tc.psum_pool(name="psum_a", bufs=4))
+        ctx.enter_context(tc.manual_schedule())
+
+        ones_f = consts.tile([P, P], F32, name="ones_f")
+        nc.gpsimd.memset(ones_f[:], 1.0)
+        ident_f = consts.tile([P, P], F32, name="ident_f")
+        make_identity(nc, ident_f[:])
+        ident_b = consts.tile([P, P], BF16, name="ident_b")
+        make_identity(nc, ident_b[:])
+        ones = consts.tile([P, P], BF16, name="ones")
+        nc.vector.memset(ones[:], 1.0)
+        zeros = consts.tile([P, 1], F32, name="zeros")
+        nc.vector.memset(zeros[:], 0.0)
+        warm = consts.tile([P, 1], F32, name="warm")
+        nc.scalar.activation(out=warm[:], in_=zeros[:], func=ACT.Sigmoid)
+
+        b2r = consts.tile([P, NCT], BF16, name="b2r")
+        with nc.allow_non_contiguous_dma(reason="512 bias values, one to a partition"):
+            nc.scalar.dma_start(out=b2r[:], in_=b2.rearrange("(c p) -> p c", p=P))
+        b2f = consts.tile([P, NCT], F32, name="b2f")
+
+        mem_sb = consts.tile([P, NMT, C], BF16, name="mem_sb")
+        memT = consts.tile([P, NCT, T], F32, name="memT")
+        q = consts.tile([P, NB * NCT], F32, name="q")
+        dmat = consts.tile([P, NMT, NCT, NB * P], F32, name="dmat")
+        wcodes = consts.tile([P, NG, C], U32, name="wcodes", align_bytes=64)
+        wscales = consts.tile([P, NG, C], U8, name="wscales", align_bytes=64)
+
+        xs_sb = {}
+        hs = {}
+        ws = {}
+        wgs = {}
+        xsums = {}
+        hgrp = {}
+        hcodes = {}
+        hscales = {}
+        accs = {}
+        gts = {}
+        tre = {}
+        oTs = {}
+        fins = {}
+        o0s = {}
+        rss = {}
+        rcs = {}
+        ams = {}
+
+        def load(src):
+            t = loads.tile([P, F], BF16, name="ld", tag="ld")
+            nc.sync.dma_start(out=t[:], in_=src)
+            return t
+
+        def load_mem():
+            nc.sync.dma_start(out=mem_sb[:], in_=memory[0].rearrange("(m r) c -> r m c", r=P))
+
+        def load_h(mt, b):
+            hs[(mt, b)] = load(h[b, mt * P:(mt + 1) * P, :])
+
+        def load_h_halves(mt, b):
+            t = loads.tile([P, F], BF16, name="ld", tag="ld")
+            for hf in range(2):
+                cols = slice(hf * (F // 2), (hf + 1) * (F // 2))
+                nc.sync.dma_start(out=t[:, cols], in_=h[b, mt * P:(mt + 1) * P, cols])
+            hs[(mt, b)] = t
+
+        def load_x(b):
+            xs_sb[b] = load(x[b].rearrange("(p j) c -> p (j c)", j=4))
+
+        def load_w(g):
+            ws[g] = load(w2[512 * g:512 * (g + 1), :].rearrange("(p j) c -> p (j c)", j=4))
+
+        def cast_b2():
+            nc.vector.tensor_copy(out=b2f[:], in_=b2r[:])
+
+        def mem_transposes():
+            for cp in range(2):
+                mp = psum_t.tile([P, 2, T], BF16, name="tp", tag="tp")
+                for c2 in range(2):
+                    ct = 2 * cp + c2
+                    for mt in range(NMT):
+                        nc.tensor.transpose(mp[:, c2, mt * P:(mt + 1) * P], mem_sb[:, mt, ct * P:(ct + 1) * P], ident_b[:])
+                if cp == 0:
+                    nc.vector.tensor_copy(out=memT[:, 0:2, :], in_=mp[:])
+                else:
+                    nc.scalar.copy(out=memT[:, 2:4, :], in_=mp[:])
+
+        def x_mm(b):
+            xt = xs_sb[b][:].rearrange("p (j c) -> p j c", j=4)
+            xsums[b] = psum_a.tile([P, NCT, XN], F32, name="acc", tag="acc")
+            for ct in range(NCT):
+                for j in range(4):
+                    nc.tensor.matmul(out=xsums[b][:, ct, :], lhsT=xt[:, j, ct * P:(ct + 1) * P], rhs=ones[:, 0:XN], start=(j == 0), stop=(j == 3))
+
+        def q_d(b):
+            nc.vector.tensor_scalar(out=q[:, NCT * b:NCT * (b + 1)], in0=xsums[b][:, :, 0], scalar1=1.0 / (T * NB), scalar2=None, op0=ALU.mult)
+            for ct in range(NCT):
+                o = dmat[:, :, ct, b * P:(b + 1) * P]
+                i = memT[:, ct, :].rearrange("p (m r) -> p m r", r=P)
+                col = q[:, NCT * b + ct:NCT * b + ct + 1]
+                if ct < 2:
+                    nc.vector.tensor_scalar(out=o, in0=i, scalar1=-0.25, scalar2=col, op0=ALU.mult, op1=ALU.add)
+                else:
+                    nc.scalar.activation(out=o, in_=i, func=ACT.Identity, bias=col, scale=-0.25)
+
+        def warm_pe(n):
+            wp = psum_a.tile([P, P], F32, name="acc", tag="acc")
+            for i in range(n):
+                nc.tensor.matmul(out=wp[:], lhsT=ones_f[:], rhs=ones_f[:], start=True, stop=True)
+
+        def t_bank(mt, b, gp, eng):
+            if mt not in hgrp:
+                hgrp[mt] = hstage.tile([P, NG, NB, P, 4], BF16, name="hgrp", tag="hgrp", align_bytes=64)
+            words = hs[(mt, b)][:].bitcast(F32)
+            tp = psum_t.tile([P, 2, 2, P], F32, name="tp", tag="tp")
+            for g2 in range(2):
+                g = 2 * gp + g2
+                for u in range(2):
+                    nc.tensor.transpose(tp[:, g2, u, :], words[:, 256 * g + u:256 * (g + 1):2], ident_f[:])
+            src = tp[:].rearrange("p g u r -> p g r u")
+            o = hgrp[mt][:].bitcast(F32)[:, 2 * gp:2 * gp + 2, b, :, :]
+            if eng == "v":
+                nc.vector.tensor_copy(out=o, in_=src)
+            else:
+                nc.scalar.copy(out=o, in_=src)
+
+        def t_tile(mt, b, engs):
+            t_bank(mt, b, 0, engs[0])
+            t_bank(mt, b, 1, engs[1])
+
+        def t_run(mt, j):
+            t_bank(mt, 2 * (j % 2), j // 2, "s")
+            t_bank(mt, 2 * (j % 2) + 1, j // 2, "s")
+
+        def quant_h(mt, g):
+            if mt not in hcodes:
+                hcodes[mt] = hstage.tile([P, NG, NB * P], U32, name="hcodes", tag="hcodes", align_bytes=64)
+                hscales[mt] = hstage.tile([P, NG, NB * P], U8, name="hscales", tag="hscales", align_bytes=64)
+            nc.vector.quantize_mx(
+                out=hcodes[mt][:, g, :].bitcast(FP8X4),
+                scales=hscales[mt][:, g, :],
+                in_=hgrp[mt][:, g].rearrange("p b r j -> p (b r j)"),
+            )
+
+        def w_interleave(g):
+            wr = ws[g][:].rearrange("p (j c) -> p c j", j=4)
+            wgs[g] = wstage.tile([P, C, 4], BF16, name="wg", tag="wg", align_bytes=64)
+            nc.vector.tensor_copy(out=wgs[g][:, 0:W_SPLIT, :], in_=wr[:, 0:W_SPLIT, :])
+            nc.scalar.copy(out=wgs[g][:, W_SPLIT:C, :], in_=wr[:, W_SPLIT:C, :])
+
+        def quant_w(g):
+            nc.vector.quantize_mx(
+                out=wcodes[:, g, :].bitcast(FP8X4),
+                scales=wscales[:, g, :],
+                in_=wgs[g][:].rearrange("p c j -> p (c j)"),
+            )
+
+        def mm(mt, ct, g):
+            if g == 0:
+                accs[(mt, ct)] = psum_a.tile([P, NB * P], F32, name="acc", tag="acc")
+            cols = slice(ct * P, (ct + 1) * P)
+            nc.tensor.matmul_mx(
+                out=accs[(mt, ct)][:],
+                lhsT=wcodes[:, g, cols].bitcast(FP8X4),
+                lhsT_scale=wscales[:, g, cols],
+                rhs=hcodes[mt][:, g, :].bitcast(FP8X4),
+                rhs_scale=hscales[mt][:, g, :],
+                start=(g == 0),
+                stop=(g == NG - 1),
+            )
+
+        def sigmoid(mt, ct):
+            if mt not in gts:
+                gts[mt] = epil.tile([P, NCT, NB * P], F32, name="gt", tag="gt")
+            nc.scalar.activation(out=gts[mt][:, ct, :], in_=accs[(mt, ct)][:], func=ACT.Sigmoid, bias=b2f[:, ct:ct + 1], scale=1.0)
+
+        def mm_ct(mt, ct):
+            for g in range(NG):
+                mm(mt, ct, g)
+            sigmoid(mt, ct)
+
+        def e_p(mt, ct):
+            gt = gts[mt]
+            nc.vector.tensor_tensor(out=gt[:, ct, :], in0=gt[:, ct, :], in1=dmat[:, mt, ct, :], op=ALU.mult)
+
+        def e_a(mt, ct):
+            if mt not in tre:
+                tre[mt] = epil.tile([P, NCT, 2 * P], F32, name="tre", tag="tre")
+            gt = gts[mt]
+            nc.vector.tensor_tensor(out=tre[mt][:, ct, :], in0=gt[:, ct, 0:2 * P], in1=gt[:, ct, 2 * P:4 * P], op=ALU.add)
+
+        def epi(mt, cts):
+            for ct in cts:
+                e_p(mt, ct)
+            for ct in cts:
+                e_a(mt, ct)
+
+        def fin_t(mt, cts, n):
+            fin = psum_a.tile([P, C], F32, name="acc", tag="acc")
+            src = tre[mt] if n == 2 else gts[mt]
+            for ct in cts:
+                fins[(mt, ct)] = fin
+                for i in range(n):
+                    nc.tensor.matmul(out=fin[:, ct * P:(ct + 1) * P], lhsT=src[:, ct, i * P:(i + 1) * P], rhs=ident_f[:], is_transpose=True, start=(i == 0), stop=(i == n - 1))
+
+        def out0(mt, c0, c1):
+            if mt not in o0s:
+                o0s[mt] = epil.tile([P, C + 4], F32, name="o0", tag="o0")
+            nc.vector.tensor_tensor(out=o0s[mt][:, c0:c1], in0=fins[(mt, c0 // P)][:, c0:c1], in1=mem_sb[:, mt, c0:c1], op=ALU.add)
+
+        def store0(mt):
+            nc.sync.dma_start(out=out_0[0, mt * P:(mt + 1) * P, :], in_=o0s[mt][:, 0:C])
+
+        def amax(mt, c0, c1, dst):
+            nc.vector.tensor_reduce(out=dst, in_=o0s[mt][:, c0:c1], axis=AX.X, op=ALU.max, apply_absolute_value=True)
+
+        def new_am(mt):
+            ams[mt] = epil.tile([P, 1], F32, name="am", tag="am")
+            return ams[mt][:]
+
+        def recip(mt):
+            rcs[mt] = epil.tile([P, 1], F32, name="rc", tag="rc")
+            nc.vector.reciprocal(out=rcs[mt][:], in_=ams[mt][:])
+
+        def r448(mt):
+            rss[mt] = epil.tile([P, 1], F32, name="rs", tag="rs")
+            nc.vector.tensor_scalar(out=rss[mt][:], in0=rcs[mt][:], scalar1=448.0, scalar2=None, op0=ALU.mult)
+
+        def cast(mt, vcols):
+            o8 = epil.tile([P, C], FP8, name="o8", tag="o8")
+            if vcols > 0:
+                nc.vector.tensor_scalar(out=o8[:, 0:vcols], in0=o0s[mt][:, 0:vcols], scalar1=rss[mt][:, 0:1], scalar2=None, op0=ALU.mult, saturate=False)
+            nc.scalar.activation(out=o8[:, vcols:C], in_=o0s[mt][:, vcols:C], func=ACT.Identity, bias=zeros[:, 0:1], scale=rss[mt][:, 0:1], saturate=False)
+            nc.sync.dma_start(out=out_1[0, mt * P:(mt + 1) * P, :], in_=o8[:].bitcast(U8))
+
+        def mm_half(hf):
+            acc = psum_a.tile([P, 2 * P], F32, name="acc", tag="acc")
+            toks = slice(hf * 2 * P, (hf + 1) * 2 * P)
+            cols = slice(3 * P, 4 * P)
+            for g in range(NG):
+                nc.tensor.matmul_mx(
+                    out=acc[:],
+                    lhsT=wcodes[:, g, cols].bitcast(FP8X4),
+                    lhsT_scale=wscales[:, g, cols],
+                    rhs=hcodes[3][:, g, toks].bitcast(FP8X4),
+                    rhs_scale=hscales[3][:, g, toks],
+                    start=(g == 0),
+                    stop=(g == NG - 1),
+                )
+            nc.scalar.activation(out=gts[3][:, 3, toks], in_=acc[:], func=ACT.Sigmoid, bias=b2f[:, 3:4], scale=1.0)
+
+        def e_p_half(hf):
+            toks = slice(hf * 2 * P, (hf + 1) * 2 * P)
+            nc.vector.tensor_tensor(out=gts[3][:, 3, toks], in0=gts[3][:, 3, toks], in1=dmat[:, 3, 3, toks], op=ALU.mult)
+
+        def fin_m(cts):
+            fin = psum_a.tile([P, C], F32, name="acc", tag="acc")
+            for ct in cts:
+                fins[(3, ct)] = fin
+                cols = slice(ct * P, (ct + 1) * P)
+                for i in range(NB):
+                    nc.tensor.matmul(out=fin[:, cols], lhsT=gts[3][:, ct, i * P:(i + 1) * P], rhs=ident_f[:], is_transpose=True, start=(i == 0), stop=False)
+                nc.tensor.matmul(out=fin[:, cols], lhsT=memT[:, ct, 3 * P:4 * P], rhs=ident_f[:], is_transpose=True, start=False, stop=True)
+
+        def copy0(c0, c1):
+            if 3 not in o0s:
+                o0s[3] = epil.tile([P, C + 4], F32, name="o0", tag="o0")
+            nc.scalar.copy(out=o0s[3][:, c0:c1], in_=fins[(3, c0 // P)][:, c0:c1])
+
+        def epi_out(mt, k):
+            e_p(mt, 0)
+            out0(k, 0, C)
+            store0(k)
+            e_p(mt, 1)
+            amax(k, 0, C, new_am(k))
+            e_a(mt, 0)
+            recip(k)
+            e_a(mt, 1)
+            r448(k)
+
+        load_h_halves(0, 0)
+        for b in range(1, NB):
+            load_h(0, b)
+        for g in range(NG):
+            load_w(g)
+            load_h(1, g)
+        load_mem()
+        for b in range(NB):
+            load_x(b)
+        for mt in (2, 3):
+            for b in range(NB):
+                load_h(mt, b)
+
+        warm_pe(7)
+        for b in range(3):
+            t_tile(0, b, "sv")
+            warm_pe(3)
+        cast_b2()
+        w_interleave(0)
+        t_tile(0, 3, "sv")
+        warm_pe(3)
+        quant_w(0)
+        quant_h(0, 0)
+        for g in range(NG):
+            if g + 1 < NG:
+                w_interleave(g + 1)
+            t_tile(1, g, "ss")
+            if g == 0:
+                warm_pe(1)
+            for ct in range(NCT):
+                mm(0, ct, g)
+            if g + 1 < NG:
+                quant_h(0, g + 1)
+                quant_w(g + 1)
+        for g in range(NG):
+            quant_h(1, g)
+        for ct in range(NCT):
+            sigmoid(0, ct)
+        mem_transposes()
+        for b in range(NB):
+            x_mm(b)
+            q_d(b)
+        t_run(2, 0)
+        mm_ct(1, 0)
+        epi(0, (0, 1))
+        t_run(2, 1)
+        mm_ct(1, 1)
+        epi(0, (2, 3))
+        t_run(2, 2)
+        mm_ct(1, 2)
+        quant_h(2, 0)
+        quant_h(2, 1)
+        fin_t(0, (0, 1, 2, 3), 2)
+        t_run(2, 3)
+        mm_ct(1, 3)
+        epi_out(1, 0)
+
+        t_run(3, 0)
+        quant_h(2, 2)
+        quant_h(2, 3)
+        mm_ct(2, 0)
+        cast(0, 0)
+        epi(1, (2, 3))
+        t_run(3, 1)
+        mm_ct(2, 1)
+        fin_t(1, (0, 1, 2, 3), 2)
+        t_run(3, 2)
+        mm_ct(2, 2)
+        quant_h(3, 0)
+        quant_h(3, 1)
+        epi_out(2, 1)
+        t_run(3, 3)
+        mm_ct(2, 3)
+        cast(1, 0)
+
+        quant_h(3, 2)
+        quant_h(3, 3)
+        mm_ct(3, 0)
+        epi(2, (2, 3))
+        mm_ct(3, 1)
+        fin_t(2, (0, 1, 2, 3), 2)
+        mm_ct(3, 2)
+        mm_half(0)
+        mm_half(1)
+
+        e_p(3, 0)
+        out0(2, 0, C)
+        store0(2)
+        e_p(3, 1)
+        amax(2, 0, C, new_am(2))
+        e_p(3, 2)
+        recip(2)
+        e_p_half(0)
+        r448(2)
+        e_p_half(1)
+        fin_m((0, 1))
+        copy0(0, 2 * P)
+        fin_m((2,))
+        copy0(2 * P, 3 * P)
+        fin_m((3,))
+        copy0(3 * P, C)
+        store0(3)
+        cast(2, 0)
+        amax(3, 0, 2 * P, o0s[3][:, C:C + 1])
+        amax(3, 2 * P, 3 * P, o0s[3][:, C + 1:C + 2])
+        amax(3, 3 * P, C + 2, new_am(3))
+        recip(3)
+        r448(3)
+        cast(3, 320)

@@ -327,19 +327,15 @@ def tile_dynamicmemorybank_pb_kernel(tc, h, x, memory, w2, b2, out_0, out_1):
         warm_pe(7)
         for b in range(3):
             t_tile(0, b, "sv")
-            warm_pe(3)
         cast_b2()
         w_interleave(0)
         t_tile(0, 3, "sv")
-        warm_pe(3)
         quant_w(0)
         quant_h(0, 0)
         for g in range(NG):
             if g + 1 < NG:
                 w_interleave(g + 1)
             t_tile(1, g, "ss")
-            if g == 0:
-                warm_pe(1)
             for ct in range(NCT):
                 mm(0, ct, g)
             if g + 1 < NG:

@@ -57,7 +57,7 @@ def tile_dynamicmemorybank_pb_kernel(tc, h, x, memory, w2, b2, out_0, out_1):
         mem_sb = consts.tile([P, NMT, C], BF16, name="mem_sb")
         memT = consts.tile([P, NCT, T], F32, name="memT")
         q = consts.tile([P, NB * NCT], F32, name="q")
-        dmat = consts.tile([P, NMT, NCT, NB * P], F32, name="dmat")
+        memT3 = consts.tile([P, NCT, P], F32, name="memT3")
         wcodes = consts.tile([P, NG, C], U32, name="wcodes", align_bytes=64)
         wscales = consts.tile([P, NG, C], U8, name="wscales", align_bytes=64)
 
@@ -113,10 +113,8 @@ def tile_dynamicmemorybank_pb_kernel(tc, h, x, memory, w2, b2, out_0, out_1):
                     ct = 2 * cp + c2
                     for mt in range(NMT):
                         nc.tensor.transpose(mp[:, c2, mt * P:(mt + 1) * P], mem_sb[:, mt, ct * P:(ct + 1) * P], ident_b[:])
-                if cp == 0:
-                    nc.vector.tensor_copy(out=memT[:, 0:2, :], in_=mp[:])
-                else:
-                    nc.scalar.copy(out=memT[:, 2:4, :], in_=mp[:])
+                nc.scalar.activation(out=memT[:, 2 * cp:2 * cp + 2, :], in_=mp[:], func=ACT.Copy, scale=-0.25)
+                nc.scalar.copy(out=memT3[:, 2 * cp:2 * cp + 2, :], in_=mp[:, :, 3 * P:4 * P])
 
         def x_mm(b):
             xt = xs_sb[b][:].rearrange("p (j c) -> p j c", j=4)
@@ -127,14 +125,6 @@ def tile_dynamicmemorybank_pb_kernel(tc, h, x, memory, w2, b2, out_0, out_1):
 
         def q_d(b):
             nc.vector.tensor_scalar(out=q[:, NCT * b:NCT * (b + 1)], in0=xsums[b][:, :, 0], scalar1=1.0 / (T * NB), scalar2=None, op0=ALU.mult)
-            for ct in range(NCT):
-                o = dmat[:, :, ct, b * P:(b + 1) * P]
-                i = memT[:, ct, :].rearrange("p (m r) -> p m r", r=P)
-                col = q[:, NCT * b + ct:NCT * b + ct + 1]
-                if ct < 2:
-                    nc.vector.tensor_scalar(out=o, in0=i, scalar1=-0.25, scalar2=col, op0=ALU.mult, op1=ALU.add)
-                else:
-                    nc.scalar.activation(out=o, in_=i, func=ACT.Identity, bias=col, scale=-0.25)
 
         def warm_pe(n):
             wp = psum_a.tile([P, P], F32, name="acc", tag="acc")
@@ -214,7 +204,8 @@ def tile_dynamicmemorybank_pb_kernel(tc, h, x, memory, w2, b2, out_0, out_1):
 
         def e_p(mt, ct):
             gt = gts[mt]
-            nc.vector.tensor_tensor(out=gt[:, ct, :], in0=gt[:, ct, :], in1=dmat[:, mt, ct, :], op=ALU.mult)
+            for b in range(NB):
+                nc.vector.scalar_tensor_tensor(out=gt[:, ct, b * P:(b + 1) * P], in0=memT[:, ct, mt * P:(mt + 1) * P], scalar=q[:, NCT * b + ct:NCT * b + ct + 1], in1=gt[:, ct, b * P:(b + 1) * P], op0=ALU.add, op1=ALU.mult)
 
         def e_a(mt, ct):
             if mt not in tre:
@@ -283,8 +274,8 @@ def tile_dynamicmemorybank_pb_kernel(tc, h, x, memory, w2, b2, out_0, out_1):
             nc.scalar.activation(out=gts[3][:, 3, toks], in_=acc[:], func=ACT.Sigmoid, bias=b2f[:, 3:4], scale=1.0)
 
         def e_p_half(hf):
-            toks = slice(hf * 2 * P, (hf + 1) * 2 * P)
-            nc.vector.tensor_tensor(out=gts[3][:, 3, toks], in0=gts[3][:, 3, toks], in1=dmat[:, 3, 3, toks], op=ALU.mult)
+            for b in (2 * hf, 2 * hf + 1):
+                nc.vector.scalar_tensor_tensor(out=gts[3][:, 3, b * P:(b + 1) * P], in0=memT[:, 3, 3 * P:4 * P], scalar=q[:, NCT * b + 3:NCT * b + 4], in1=gts[3][:, 3, b * P:(b + 1) * P], op0=ALU.add, op1=ALU.mult)
 
         def fin_m(cts):
             fin = psum_a.tile([P, C], F32, name="acc", tag="acc")
@@ -293,7 +284,7 @@ def tile_dynamicmemorybank_pb_kernel(tc, h, x, memory, w2, b2, out_0, out_1):
                 cols = slice(ct * P, (ct + 1) * P)
                 for i in range(NB):
                     nc.tensor.matmul(out=fin[:, cols], lhsT=gts[3][:, ct, i * P:(i + 1) * P], rhs=ident_f[:], is_transpose=True, start=(i == 0), stop=False)
-                nc.tensor.matmul(out=fin[:, cols], lhsT=memT[:, ct, 3 * P:4 * P], rhs=ident_f[:], is_transpose=True, start=False, stop=True)
+                nc.tensor.matmul(out=fin[:, cols], lhsT=memT3[:, ct, :], rhs=ident_f[:], is_transpose=True, start=False, stop=True)
 
         def copy0(c0, c1):
             if 3 not in o0s:
@@ -309,6 +300,17 @@ def tile_dynamicmemorybank_pb_kernel(tc, h, x, memory, w2, b2, out_0, out_1):
             e_a(mt, 0)
             recip(k)
             e_a(mt, 1)
+            r448(k)
+
+        def epi_out2(mt, k):
+            e_p(mt, 2)
+            out0(k, 0, C)
+            store0(k)
+            e_p(mt, 3)
+            amax(k, 0, C, new_am(k))
+            e_a(mt, 2)
+            recip(k)
+            e_a(mt, 3)
             r448(k)
 
         load_h_halves(0, 0)
@@ -349,46 +351,45 @@ def tile_dynamicmemorybank_pb_kernel(tc, h, x, memory, w2, b2, out_0, out_1):
         for b in range(NB):
             x_mm(b)
             q_d(b)
-        t_run(2, 0)
         mm_ct(1, 0)
-        epi(0, (0, 1))
-        t_run(2, 1)
         mm_ct(1, 1)
+        epi(0, (0, 1))
+        t_tile(2, 0, "ss")
+        t_tile(2, 1, "ss")
         epi(0, (2, 3))
-        t_run(2, 2)
         mm_ct(1, 2)
+        t_tile(2, 2, "ss")
+        t_tile(2, 3, "ss")
+        epi(1, (0, 1))
+        mm_ct(1, 3)
+        fin_t(0, (0, 1, 2, 3), 2)
+        t_run(3, 0)
         quant_h(2, 0)
         quant_h(2, 1)
-        fin_t(0, (0, 1, 2, 3), 2)
-        t_run(2, 3)
-        mm_ct(1, 3)
-        epi_out(1, 0)
-
-        t_run(3, 0)
         quant_h(2, 2)
         quant_h(2, 3)
+        epi_out2(1, 0)
         mm_ct(2, 0)
-        cast(0, 0)
-        epi(1, (2, 3))
         t_run(3, 1)
-        mm_ct(2, 1)
-        fin_t(1, (0, 1, 2, 3), 2)
         t_run(3, 2)
-        mm_ct(2, 2)
+        cast(0, 0)
+        mm_ct(2, 1)
         quant_h(3, 0)
         quant_h(3, 1)
-        epi_out(2, 1)
+        fin_t(1, (0, 1, 2, 3), 2)
         t_run(3, 3)
-        mm_ct(2, 3)
-        cast(1, 0)
-
+        epi(2, (0, 1))
+        mm_ct(2, 2)
         quant_h(3, 2)
         quant_h(3, 3)
+        mm_ct(2, 3)
+        epi_out2(2, 1)
+
         mm_ct(3, 0)
-        epi(2, (2, 3))
         mm_ct(3, 1)
-        fin_t(2, (0, 1, 2, 3), 2)
+        cast(1, 0)
         mm_ct(3, 2)
+        fin_t(2, (0, 1, 2, 3), 2)
         mm_half(0)
         mm_half(1)
 

@@ -31,6 +31,7 @@ def tile_dynamicmemorybank_pb_kernel(tc, h, x, memory, w2, b2, out_0, out_1):
         loads = ctx.enter_context(tc.tile_pool(name="loads", bufs=16))
         wstage = ctx.enter_context(tc.tile_pool(name="wstage", bufs=2))
         hstage = ctx.enter_context(tc.tile_pool(name="hstage", bufs=2))
+        dstage = ctx.enter_context(tc.tile_pool(name="dstage", bufs=4))
         epil = ctx.enter_context(tc.tile_pool(name="epil", bufs=2))
         psum_t = ctx.enter_context(tc.psum_pool(name="psum_t", bufs=4))
         psum_a = ctx.enter_context(tc.psum_pool(name="psum_a", bufs=4))
@@ -63,6 +64,7 @@ def tile_dynamicmemorybank_pb_kernel(tc, h, x, memory, w2, b2, out_0, out_1):
 
         xs_sb = {}
         hs = {}
+        hds = {}
         ws = {}
         wgs = {}
         xsums = {}
@@ -131,15 +133,29 @@ def tile_dynamicmemorybank_pb_kernel(tc, h, x, memory, w2, b2, out_0, out_1):
             for i in range(n):
                 nc.tensor.matmul(out=wp[:], lhsT=ones_f[:], rhs=ones_f[:], start=True, stop=True)
 
+        def deint(mt, b, eng):
+            hd = dstage.tile([P, F], BF16, name="hd", tag="hd")
+            o = hd[:].bitcast(F32).rearrange("p (g u w) -> p g u w", g=NG, u=2)
+            i = hs[(mt, b)][:].bitcast(F32).rearrange("p (g w u) -> p g u w", g=NG, u=2)
+            if eng == "v":
+                nc.vector.tensor_copy(out=o, in_=i)
+            else:
+                nc.scalar.copy(out=o, in_=i)
+            hds[(mt, b)] = hd
+
         def t_bank(mt, b, gp, eng):
             if mt not in hgrp:
                 hgrp[mt] = hstage.tile([P, NG, NB, P, 4], BF16, name="hgrp", tag="hgrp", align_bytes=64)
-            words = hs[(mt, b)][:].bitcast(F32)
+            dense = (mt, b) in hds
+            words = (hds[(mt, b)] if dense else hs[(mt, b)])[:].bitcast(F32)
             tp = psum_t.tile([P, 2, 2, P], F32, name="tp", tag="tp")
             for g2 in range(2):
                 g = 2 * gp + g2
                 for u in range(2):
-                    nc.tensor.transpose(tp[:, g2, u, :], words[:, 256 * g + u:256 * (g + 1):2], ident_f[:])
+                    if dense:
+                        nc.tensor.transpose(tp[:, g2, u, :], words[:, 256 * g + 128 * u:256 * g + 128 * (u + 1)], ident_f[:])
+                    else:
+                        nc.tensor.transpose(tp[:, g2, u, :], words[:, 256 * g + u:256 * (g + 1):2], ident_f[:])
             src = tp[:].rearrange("p g u r -> p g r u")
             o = hgrp[mt][:].bitcast(F32)[:, 2 * gp:2 * gp + 2, b, :, :]
             if eng == "v":
@@ -361,6 +377,9 @@ def tile_dynamicmemorybank_pb_kernel(tc, h, x, memory, w2, b2, out_0, out_1):
         t_tile(2, 2, "ss")
         t_tile(2, 3, "ss")
         epi(1, (0, 1))
+        deint(3, 0, "v")
+        deint(3, 1, "v")
+        deint(3, 2, "v")
         mm_ct(1, 3)
         fin_t(0, (0, 1, 2, 3), 2)
         t_run(3, 0)
@@ -368,6 +387,7 @@ def tile_dynamicmemorybank_pb_kernel(tc, h, x, memory, w2, b2, out_0, out_1):
         quant_h(2, 1)
         quant_h(2, 2)
         quant_h(2, 3)
+        deint(3, 3, "v")
         epi_out2(1, 0)
         mm_ct(2, 0)
         t_run(3, 1)
@@ -378,12 +398,20 @@ def tile_dynamicmemorybank_pb_kernel(tc, h, x, memory, w2, b2, out_0, out_1):
         quant_h(3, 1)
         fin_t(1, (0, 1, 2, 3), 2)
         t_run(3, 3)
-        epi(2, (0, 1))
+        e_p(2, 0)
+        out0(1, 0, C)
+        store0(1)
+        e_p(2, 1)
+        amax(1, 0, C, new_am(1))
         mm_ct(2, 2)
         quant_h(3, 2)
         quant_h(3, 3)
+        recip(1)
+        e_a(2, 0)
+        r448(1)
+        e_a(2, 1)
         mm_ct(2, 3)
-        epi_out2(2, 1)
+        epi(2, (2, 3))
 
         mm_ct(3, 0)
         mm_ct(3, 1)

@@ -31,7 +31,7 @@ def tile_dynamicmemorybank_pb_kernel(tc, h, x, memory, w2, b2, out_0, out_1):
         loads = ctx.enter_context(tc.tile_pool(name="loads", bufs=16))
         wstage = ctx.enter_context(tc.tile_pool(name="wstage", bufs=2))
         hstage = ctx.enter_context(tc.tile_pool(name="hstage", bufs=2))
-        dstage = ctx.enter_context(tc.tile_pool(name="dstage", bufs=4))
+        dstage = ctx.enter_context(tc.tile_pool(name="dstage", bufs=6))
         epil = ctx.enter_context(tc.tile_pool(name="epil", bufs=2))
         psum_t = ctx.enter_context(tc.psum_pool(name="psum_t", bufs=4))
         psum_a = ctx.enter_context(tc.psum_pool(name="psum_a", bufs=4))
@@ -58,7 +58,7 @@ def tile_dynamicmemorybank_pb_kernel(tc, h, x, memory, w2, b2, out_0, out_1):
         mem_sb = consts.tile([P, NMT, C], BF16, name="mem_sb")
         memT = consts.tile([P, NCT, T], F32, name="memT")
         q = consts.tile([P, NB * NCT], F32, name="q")
-        memT3 = consts.tile([P, NCT, P], F32, name="memT3")
+        memT3 = consts.tile([P, NCT, 2 * P], F32, name="memT3")
         wcodes = consts.tile([P, NG, C], U32, name="wcodes", align_bytes=64)
         wscales = consts.tile([P, NG, C], U8, name="wscales", align_bytes=64)
 
@@ -116,7 +116,7 @@ def tile_dynamicmemorybank_pb_kernel(tc, h, x, memory, w2, b2, out_0, out_1):
                     for mt in range(NMT):
                         nc.tensor.transpose(mp[:, c2, mt * P:(mt + 1) * P], mem_sb[:, mt, ct * P:(ct + 1) * P], ident_b[:])
                 nc.scalar.activation(out=memT[:, 2 * cp:2 * cp + 2, :], in_=mp[:], func=ACT.Copy, scale=-0.25)
-                nc.scalar.copy(out=memT3[:, 2 * cp:2 * cp + 2, :], in_=mp[:, :, 3 * P:4 * P])
+                nc.scalar.copy(out=memT3[:, 2 * cp:2 * cp + 2, :], in_=mp[:, :, 2 * P:4 * P])
 
         def x_mm(b):
             xt = xs_sb[b][:].rearrange("p (j c) -> p j c", j=4)
@@ -293,19 +293,20 @@ def tile_dynamicmemorybank_pb_kernel(tc, h, x, memory, w2, b2, out_0, out_1):
             for b in (2 * hf, 2 * hf + 1):
                 nc.vector.scalar_tensor_tensor(out=gts[3][:, 3, b * P:(b + 1) * P], in0=memT[:, 3, 3 * P:4 * P], scalar=q[:, NCT * b + 3:NCT * b + 4], in1=gts[3][:, 3, b * P:(b + 1) * P], op0=ALU.add, op1=ALU.mult)
 
-        def fin_m(cts):
+        def fin_m(mt, cts, n):
             fin = psum_a.tile([P, C], F32, name="acc", tag="acc")
+            src = tre[mt] if n == 2 else gts[mt]
             for ct in cts:
-                fins[(3, ct)] = fin
+                fins[(mt, ct)] = fin
                 cols = slice(ct * P, (ct + 1) * P)
-                for i in range(NB):
-                    nc.tensor.matmul(out=fin[:, cols], lhsT=gts[3][:, ct, i * P:(i + 1) * P], rhs=ident_f[:], is_transpose=True, start=(i == 0), stop=False)
-                nc.tensor.matmul(out=fin[:, cols], lhsT=memT3[:, ct, :], rhs=ident_f[:], is_transpose=True, start=False, stop=True)
+                for i in range(n):
+                    nc.tensor.matmul(out=fin[:, cols], lhsT=src[:, ct, i * P:(i + 1) * P], rhs=ident_f[:], is_transpose=True, start=(i == 0), stop=False)
+                nc.tensor.matmul(out=fin[:, cols], lhsT=memT3[:, ct, (mt - 2) * P:(mt - 1) * P], rhs=ident_f[:], is_transpose=True, start=False, stop=True)
 
-        def copy0(c0, c1):
-            if 3 not in o0s:
-                o0s[3] = epil.tile([P, C + 4], F32, name="o0", tag="o0")
-            nc.scalar.copy(out=o0s[3][:, c0:c1], in_=fins[(3, c0 // P)][:, c0:c1])
+        def copy0(mt, c0, c1):
+            if mt not in o0s:
+                o0s[mt] = epil.tile([P, C + 4], F32, name="o0", tag="o0")
+            nc.scalar.copy(out=o0s[mt][:, c0:c1], in_=fins[(mt, c0 // P)][:, c0:c1])
 
         def epi_out(mt, k):
             e_p(mt, 0)
@@ -372,7 +373,11 @@ def tile_dynamicmemorybank_pb_kernel(tc, h, x, memory, w2, b2, out_0, out_1):
         epi(0, (0, 1))
         t_tile(2, 0, "ss")
         t_tile(2, 1, "ss")
-        epi(0, (2, 3))
+        e_p(0, 2)
+        e_p(0, 3)
+        deint(2, 3, "v")
+        e_a(0, 2)
+        e_a(0, 3)
         mm_ct(1, 2)
         t_tile(2, 2, "ss")
         t_tile(2, 3, "ss")
@@ -380,6 +385,7 @@ def tile_dynamicmemorybank_pb_kernel(tc, h, x, memory, w2, b2, out_0, out_1):
         deint(3, 0, "v")
         deint(3, 1, "v")
         deint(3, 2, "v")
+        deint(3, 3, "s")
         mm_ct(1, 3)
         fin_t(0, (0, 1, 2, 3), 2)
         t_run(3, 0)
@@ -387,7 +393,6 @@ def tile_dynamicmemorybank_pb_kernel(tc, h, x, memory, w2, b2, out_0, out_1):
         quant_h(2, 1)
         quant_h(2, 2)
         quant_h(2, 3)
-        deint(3, 3, "v")
         epi_out2(1, 0)
         mm_ct(2, 0)
         t_run(3, 1)
@@ -417,26 +422,26 @@ def tile_dynamicmemorybank_pb_kernel(tc, h, x, memory, w2, b2, out_0, out_1):
         mm_ct(3, 1)
         cast(1, 0)
         mm_ct(3, 2)
-        fin_t(2, (0, 1, 2, 3), 2)
+        fin_m(2, (0, 1, 2, 3), 2)
+        copy0(2, 0, C)
+        store0(2)
         mm_half(0)
         mm_half(1)
 
         e_p(3, 0)
-        out0(2, 0, C)
-        store0(2)
         e_p(3, 1)
-        amax(2, 0, C, new_am(2))
         e_p(3, 2)
-        recip(2)
+        amax(2, 0, C, new_am(2))
         e_p_half(0)
-        r448(2)
+        recip(2)
         e_p_half(1)
-        fin_m((0, 1))
-        copy0(0, 2 * P)
-        fin_m((2,))
-        copy0(2 * P, 3 * P)
-        fin_m((3,))
-        copy0(3 * P, C)
+        r448(2)
+        fin_m(3, (0, 1), 4)
+        copy0(3, 0, 2 * P)
+        fin_m(3, (2,), 4)
+        copy0(3, 2 * P, 3 * P)
+        fin_m(3, (3,), 4)
+        copy0(3, 3 * P, C)
         store0(3)
         cast(2, 0)
         amax(3, 0, 2 * P, o0s[3][:, C:C + 1])

@@ -31,7 +31,7 @@ def tile_dynamicmemorybank_pb_kernel(tc, h, x, memory, w2, b2, out_0, out_1):
         loads = ctx.enter_context(tc.tile_pool(name="loads", bufs=16))
         wstage = ctx.enter_context(tc.tile_pool(name="wstage", bufs=2))
         hstage = ctx.enter_context(tc.tile_pool(name="hstage", bufs=2))
-        dstage = ctx.enter_context(tc.tile_pool(name="dstage", bufs=6))
+        dstage = ctx.enter_context(tc.tile_pool(name="dstage", bufs=8))
         epil = ctx.enter_context(tc.tile_pool(name="epil", bufs=2))
         psum_t = ctx.enter_context(tc.psum_pool(name="psum_t", bufs=4))
         psum_a = ctx.enter_context(tc.psum_pool(name="psum_a", bufs=4))
@@ -115,8 +115,13 @@ def tile_dynamicmemorybank_pb_kernel(tc, h, x, memory, w2, b2, out_0, out_1):
                     ct = 2 * cp + c2
                     for mt in range(NMT):
                         nc.tensor.transpose(mp[:, c2, mt * P:(mt + 1) * P], mem_sb[:, mt, ct * P:(ct + 1) * P], ident_b[:])
-                nc.scalar.activation(out=memT[:, 2 * cp:2 * cp + 2, :], in_=mp[:], func=ACT.Copy, scale=-0.25)
-                nc.scalar.copy(out=memT3[:, 2 * cp:2 * cp + 2, :], in_=mp[:, :, 2 * P:4 * P])
+                if cp == 0:
+                    nc.vector.tensor_scalar(out=memT[:, 0:2, :], in0=mp[:], scalar1=-0.25, scalar2=None, op0=ALU.mult)
+                else:
+                    nc.scalar.activation(out=memT[:, 2:4, :], in_=mp[:], func=ACT.Copy, scale=-0.25)
+
+        def mem3():
+            nc.scalar.activation(out=memT3[:], in_=memT[:, :, 2 * P:4 * P], func=ACT.Copy, scale=-4.0)
 
         def x_mm(b):
             xt = xs_sb[b][:].rearrange("p (j c) -> p j c", j=4)
@@ -222,6 +227,17 @@ def tile_dynamicmemorybank_pb_kernel(tc, h, x, memory, w2, b2, out_0, out_1):
             gt = gts[mt]
             for b in range(NB):
                 nc.vector.scalar_tensor_tensor(out=gt[:, ct, b * P:(b + 1) * P], in0=memT[:, ct, mt * P:(mt + 1) * P], scalar=q[:, NCT * b + ct:NCT * b + ct + 1], in1=gt[:, ct, b * P:(b + 1) * P], op0=ALU.add, op1=ALU.mult)
+
+        def e_pb(mt, b):
+            gt = gts[mt]
+            for ct in range(NCT):
+                nc.vector.scalar_tensor_tensor(out=gt[:, ct, b * P:(b + 1) * P], in0=memT[:, ct, mt * P:(mt + 1) * P], scalar=q[:, NCT * b + ct:NCT * b + ct + 1], in1=gt[:, ct, b * P:(b + 1) * P], op0=ALU.add, op1=ALU.mult)
+
+        def e_pc(mt, cts, bs):
+            gt = gts[mt]
+            for b in bs:
+                for ct in cts:
+                    nc.vector.scalar_tensor_tensor(out=gt[:, ct, b * P:(b + 1) * P], in0=memT[:, ct, mt * P:(mt + 1) * P], scalar=q[:, NCT * b + ct:NCT * b + ct + 1], in1=gt[:, ct, b * P:(b + 1) * P], op0=ALU.add, op1=ALU.mult)
 
         def e_a(mt, ct):
             if mt not in tre:
@@ -365,23 +381,34 @@ def tile_dynamicmemorybank_pb_kernel(tc, h, x, memory, w2, b2, out_0, out_1):
         for ct in range(NCT):
             sigmoid(0, ct)
         mem_transposes()
+        mem3()
         for b in range(NB):
             x_mm(b)
-            q_d(b)
+        q_d(0)
+        q_d(1)
+        e_pc(0, (0, 1), (0, 1))
+        q_d(2)
+        e_pc(0, (2, 3), (0, 1))
+        e_pc(0, (0, 1, 2, 3), (2,))
+        deint(2, 0, "s")
+        q_d(3)
+        e_pc(0, (0, 1, 2, 3), (3,))
         mm_ct(1, 0)
         mm_ct(1, 1)
-        epi(0, (0, 1))
+        e_a(0, 0)
+        e_a(0, 1)
         t_tile(2, 0, "ss")
         t_tile(2, 1, "ss")
-        e_p(0, 2)
-        e_p(0, 3)
-        deint(2, 3, "v")
         e_a(0, 2)
         e_a(0, 3)
+        e_p(1, 0)
+        deint(2, 3, "v")
         mm_ct(1, 2)
         t_tile(2, 2, "ss")
         t_tile(2, 3, "ss")
-        epi(1, (0, 1))
+        e_p(1, 1)
+        e_a(1, 0)
+        e_a(1, 1)
         deint(3, 0, "v")
         deint(3, 1, "v")
         deint(3, 2, "v")

@@ -59,8 +59,8 @@ def tile_dynamicmemorybank_pb_kernel(tc, h, x, memory, w2, b2, out_0, out_1):
         memT = consts.tile([P, NCT, T], F32, name="memT")
         q = consts.tile([P, NB * NCT], F32, name="q")
         memT3 = consts.tile([P, NCT, 2 * P], F32, name="memT3")
-        wcodes = consts.tile([P, NG, C], U32, name="wcodes", align_bytes=64)
-        wscales = consts.tile([P, NG, C], U8, name="wscales", align_bytes=64)
+        wcodes = consts.tile([P, NG, C], U32, name="wcodes", align_bytes=256)
+        wscales = consts.tile([P, NG, C], U8, name="wscales", align_bytes=256)
 
         xs_sb = {}
         hs = {}
@@ -178,8 +178,8 @@ def tile_dynamicmemorybank_pb_kernel(tc, h, x, memory, w2, b2, out_0, out_1):
 
         def quant_h(mt, g):
             if mt not in hcodes:
-                hcodes[mt] = hstage.tile([P, NG, NB * P], U32, name="hcodes", tag="hcodes", align_bytes=64)
-                hscales[mt] = hstage.tile([P, NG, NB * P], U8, name="hscales", tag="hscales", align_bytes=64)
+                hcodes[mt] = hstage.tile([P, NG, NB * P], U32, name="hcodes", tag="hcodes", align_bytes=256)
+                hscales[mt] = hstage.tile([P, NG, NB * P], U8, name="hscales", tag="hscales", align_bytes=256)
             nc.vector.quantize_mx(
                 out=hcodes[mt][:, g, :].bitcast(FP8X4),
                 scales=hscales[mt][:, g, :],

@@ -37,13 +37,13 @@ def tile_dynamicmemorybank_pb_kernel(tc, h, x, memory, w2, b2, out_0, out_1):
         psum_a = ctx.enter_context(tc.psum_pool(name="psum_a", bufs=4))
         ctx.enter_context(tc.manual_schedule())
 
-        ones_f = consts.tile([P, P], F32, name="ones_f")
+        ones_f = consts.tile([P, P], F32, name="ones_f", align_bytes=256)
         nc.gpsimd.memset(ones_f[:], 1.0)
-        ident_f = consts.tile([P, P], F32, name="ident_f")
+        ident_f = consts.tile([P, P], F32, name="ident_f", align_bytes=256)
         make_identity(nc, ident_f[:])
-        ident_b = consts.tile([P, P], BF16, name="ident_b")
+        ident_b = consts.tile([P, P], BF16, name="ident_b", align_bytes=256)
         make_identity(nc, ident_b[:])
-        ones = consts.tile([P, P], BF16, name="ones")
+        ones = consts.tile([P, P], BF16, name="ones", align_bytes=256)
         nc.vector.memset(ones[:], 1.0)
         zeros = consts.tile([P, 1], F32, name="zeros")
         nc.vector.memset(zeros[:], 0.0)
@@ -55,10 +55,10 @@ def tile_dynamicmemorybank_pb_kernel(tc, h, x, memory, w2, b2, out_0, out_1):
             nc.scalar.dma_start(out=b2r[:], in_=b2.rearrange("(c p) -> p c", p=P))
         b2f = consts.tile([P, NCT], F32, name="b2f")
 
-        mem_sb = consts.tile([P, NMT, C], BF16, name="mem_sb")
-        memT = consts.tile([P, NCT, T], F32, name="memT")
+        mem_sb = consts.tile([P, NMT, C], BF16, name="mem_sb", align_bytes=256)
+        memT = consts.tile([P, NCT, T], F32, name="memT", align_bytes=256)
         q = consts.tile([P, NB * NCT], F32, name="q")
-        memT3 = consts.tile([P, NCT, 2 * P], F32, name="memT3")
+        memT3 = consts.tile([P, NCT, 2 * P], F32, name="memT3", align_bytes=256)
         wcodes = consts.tile([P, NG, C], U32, name="wcodes", align_bytes=256)
         wscales = consts.tile([P, NG, C], U8, name="wscales", align_bytes=256)
 
@@ -82,7 +82,7 @@ def tile_dynamicmemorybank_pb_kernel(tc, h, x, memory, w2, b2, out_0, out_1):
         ams = {}
 
         def load(src):
-            t = loads.tile([P, F], BF16, name="ld", tag="ld")
+            t = loads.tile([P, F], BF16, name="ld", tag="ld", align_bytes=256)
             nc.sync.dma_start(out=t[:], in_=src)
             return t
 
@@ -93,7 +93,7 @@ def tile_dynamicmemorybank_pb_kernel(tc, h, x, memory, w2, b2, out_0, out_1):
             hs[(mt, b)] = load(h[b, mt * P:(mt + 1) * P, :])
 
         def load_h_halves(mt, b):
-            t = loads.tile([P, F], BF16, name="ld", tag="ld")
+            t = loads.tile([P, F], BF16, name="ld", tag="ld", align_bytes=256)
             for hf in range(2):
                 cols = slice(hf * (F // 2), (hf + 1) * (F // 2))
                 nc.sync.dma_start(out=t[:, cols], in_=h[b, mt * P:(mt + 1) * P, cols])
@@ -139,7 +139,7 @@ def tile_dynamicmemorybank_pb_kernel(tc, h, x, memory, w2, b2, out_0, out_1):
                 nc.tensor.matmul(out=wp[:], lhsT=ones_f[:], rhs=ones_f[:], start=True, stop=True)
 
         def deint(mt, b, eng):
-            hd = dstage.tile([P, F], BF16, name="hd", tag="hd")
+            hd = dstage.tile([P, F], BF16, name="hd", tag="hd", align_bytes=256)
             o = hd[:].bitcast(F32).rearrange("p (g u w) -> p g u w", g=NG, u=2)
             i = hs[(mt, b)][:].bitcast(F32).rearrange("p (g w u) -> p g u w", g=NG, u=2)
             if eng == "v":
@@ -150,7 +150,7 @@ def tile_dynamicmemorybank_pb_kernel(tc, h, x, memory, w2, b2, out_0, out_1):
 
         def t_bank(mt, b, gp, eng):
             if mt not in hgrp:
-                hgrp[mt] = hstage.tile([P, NG, NB, P, 4], BF16, name="hgrp", tag="hgrp", align_bytes=64)
+                hgrp[mt] = hstage.tile([P, NG, NB, P, 4], BF16, name="hgrp", tag="hgrp", align_bytes=256)
             dense = (mt, b) in hds
             words = (hds[(mt, b)] if dense else hs[(mt, b)])[:].bitcast(F32)
             tp = psum_t.tile([P, 2, 2, P], F32, name="tp", tag="tp")
@@ -188,7 +188,7 @@ def tile_dynamicmemorybank_pb_kernel(tc, h, x, memory, w2, b2, out_0, out_1):
 
         def w_interleave(g):
             wr = ws[g][:].rearrange("p (j c) -> p c j", j=4)
-            wgs[g] = wstage.tile([P, C, 4], BF16, name="wg", tag="wg", align_bytes=64)
+            wgs[g] = wstage.tile([P, C, 4], BF16, name="wg", tag="wg", align_bytes=256)
             nc.vector.tensor_copy(out=wgs[g][:, 0:W_SPLIT, :], in_=wr[:, 0:W_SPLIT, :])
             nc.scalar.copy(out=wgs[g][:, W_SPLIT:C, :], in_=wr[:, W_SPLIT:C, :])
 
@@ -215,7 +215,7 @@ def tile_dynamicmemorybank_pb_kernel(tc, h, x, memory, w2, b2, out_0, out_1):
 
         def sigmoid(mt, ct):
             if mt not in gts:
-                gts[mt] = epil.tile([P, NCT, NB * P], F32, name="gt", tag="gt")
+                gts[mt] = epil.tile([P, NCT, NB * P], F32, name="gt", tag="gt", align_bytes=256)
             nc.scalar.activation(out=gts[mt][:, ct, :], in_=accs[(mt, ct)][:], func=ACT.Sigmoid, bias=b2f[:, ct:ct + 1], scale=1.0)
 
         def mm_ct(mt, ct):
@@ -241,7 +241,7 @@ def tile_dynamicmemorybank_pb_kernel(tc, h, x, memory, w2, b2, out_0, out_1):
 
         def e_a(mt, ct):
             if mt not in tre:
-                tre[mt] = epil.tile([P, NCT, 2 * P], F32, name="tre", tag="tre")
+                tre[mt] = epil.tile([P, NCT, 2 * P], F32, name="tre", tag="tre", align_bytes=256)
             gt = gts[mt]
             nc.vector.tensor_tensor(out=tre[mt][:, ct, :], in0=gt[:, ct, 0:2 * P], in1=gt[:, ct, 2 * P:4 * P], op=ALU.add)
 
@@ -261,7 +261,7 @@ def tile_dynamicmemorybank_pb_kernel(tc, h, x, memory, w2, b2, out_0, out_1):
 
         def out0(mt, c0, c1):
             if mt not in o0s:
-                o0s[mt] = epil.tile([P, C + 4], F32, name="o0", tag="o0")
+                o0s[mt] = epil.tile([P, C + 4], F32, name="o0", tag="o0", align_bytes=256)
             nc.vector.tensor_tensor(out=o0s[mt][:, c0:c1], in0=fins[(mt, c0 // P)][:, c0:c1], in1=mem_sb[:, mt, c0:c1], op=ALU.add)
 
         def store0(mt):
@@ -283,7 +283,7 @@ def tile_dynamicmemorybank_pb_kernel(tc, h, x, memory, w2, b2, out_0, out_1):
             nc.vector.tensor_scalar(out=rss[mt][:], in0=rcs[mt][:], scalar1=448.0, scalar2=None, op0=ALU.mult)
 
         def cast(mt, vcols):
-            o8 = epil.tile([P, C], FP8, name="o8", tag="o8")
+            o8 = epil.tile([P, C], FP8, name="o8", tag="o8", align_bytes=256)
             if vcols > 0:
                 nc.vector.tensor_scalar(out=o8[:, 0:vcols], in0=o0s[mt][:, 0:vcols], scalar1=rss[mt][:, 0:1], scalar2=None, op0=ALU.mult, saturate=False)
             nc.scalar.activation(out=o8[:, vcols:C], in_=o0s[mt][:, vcols:C], func=ACT.Identity, bias=zeros[:, 0:1], scale=rss[mt][:, 0:1], saturate=False)
@@ -321,7 +321,7 @@ def tile_dynamicmemorybank_pb_kernel(tc, h, x, memory, w2, b2, out_0, out_1):
 
         def copy0(mt, c0, c1):
             if mt not in o0s:
-                o0s[mt] = epil.tile([P, C + 4], F32, name="o0", tag="o0")
+                o0s[mt] = epil.tile([P, C + 4], F32, name="o0", tag="o0", align_bytes=256)
             nc.scalar.copy(out=o0s[mt][:, c0:c1], in_=fins[(mt, c0 // P)][:, c0:c1])
 
         def epi_out(mt, k):

@@ -20,7 +20,7 @@ NCT = C // P
 NG = F // 512
 FLOPS = 2 * NB * T * F * C
 
-XN = 64
+XN = 32
 W_SPLIT = 320
 
 

@@ -43,6 +43,7 @@ def tile_dynamicmemorybank_pb_kernel(tc, h, x, memory, w2, b2, out_0, out_1):
         make_identity(nc, ident_f[:])
         ident_b = consts.tile([P, P], BF16, name="ident_b", align_bytes=256)
         make_identity(nc, ident_b[:])
+        neg4 = consts.tile([P, P], BF16, name="neg4", align_bytes=256)
         ones = consts.tile([P, P], BF16, name="ones", align_bytes=256)
         nc.vector.memset(ones[:], 1.0)
         zeros = consts.tile([P, 1], F32, name="zeros")
@@ -56,9 +57,8 @@ def tile_dynamicmemorybank_pb_kernel(tc, h, x, memory, w2, b2, out_0, out_1):
         b2f = consts.tile([P, NCT], F32, name="b2f")
 
         mem_sb = consts.tile([P, NMT, C], BF16, name="mem_sb", align_bytes=256)
-        memT = consts.tile([P, NCT, T], F32, name="memT", align_bytes=256)
+        memT = consts.tile([P, NCT, T], BF16, name="memT", align_bytes=256)
         q = consts.tile([P, NB * NCT], F32, name="q")
-        memT3 = consts.tile([P, NCT, 2 * P], F32, name="memT3", align_bytes=256)
         wcodes = consts.tile([P, NG, C], U32, name="wcodes", align_bytes=256)
         wscales = consts.tile([P, NG, C], U8, name="wscales", align_bytes=256)
 
@@ -107,6 +107,7 @@ def tile_dynamicmemorybank_pb_kernel(tc, h, x, memory, w2, b2, out_0, out_1):
 
         def cast_b2():
             nc.vector.tensor_copy(out=b2f[:], in_=b2r[:])
+            nc.vector.tensor_scalar(out=neg4[:], in0=ident_b[:], scalar1=-4.0, scalar2=None, op0=ALU.mult)
 
         def mem_transposes():
             for cp in range(2):
@@ -116,12 +117,9 @@ def tile_dynamicmemorybank_pb_kernel(tc, h, x, memory, w2, b2, out_0, out_1):
                     for mt in range(NMT):
                         nc.tensor.transpose(mp[:, c2, mt * P:(mt + 1) * P], mem_sb[:, mt, ct * P:(ct + 1) * P], ident_b[:])
                 if cp == 0:
-                    nc.vector.tensor_scalar(out=memT[:, 0:2, :], in0=mp[:], scalar1=-0.25, scalar2=None, op0=ALU.mult)
+                    nc.vector.tensor_copy(out=memT[:, 0:2, :], in_=mp[:])
                 else:
-                    nc.scalar.activation(out=memT[:, 2:4, :], in_=mp[:], func=ACT.Copy, scale=-0.25)
-
-        def mem3():
-            nc.scalar.activation(out=memT3[:], in_=memT[:, :, 2 * P:4 * P], func=ACT.Copy, scale=-4.0)
+                    nc.scalar.copy(out=memT[:, 2:4, :], in_=mp[:])
 
         def x_mm(b):
             xt = xs_sb[b][:].rearrange("p (j c) -> p j c", j=4)
@@ -131,7 +129,7 @@ def tile_dynamicmemorybank_pb_kernel(tc, h, x, memory, w2, b2, out_0, out_1):
                     nc.tensor.matmul(out=xsums[b][:, ct, :], lhsT=xt[:, j, ct * P:(ct + 1) * P], rhs=ones[:, 0:XN], start=(j == 0), stop=(j == 3))
 
         def q_d(b):
-            nc.vector.tensor_scalar(out=q[:, NCT * b:NCT * (b + 1)], in0=xsums[b][:, :, 0], scalar1=1.0 / (T * NB), scalar2=None, op0=ALU.mult)
+            nc.vector.tensor_scalar(out=q[:, NCT * b:NCT * (b + 1)], in0=xsums[b][:, :, 0], scalar1=1.0 / T, scalar2=None, op0=ALU.mult)
 
         def warm_pe(n):
             wp = psum_a.tile([P, P], F32, name="acc", tag="acc")
@@ -226,18 +224,18 @@ def tile_dynamicmemorybank_pb_kernel(tc, h, x, memory, w2, b2, out_0, out_1):
         def e_p(mt, ct):
             gt = gts[mt]
             for b in range(NB):
-                nc.vector.scalar_tensor_tensor(out=gt[:, ct, b * P:(b + 1) * P], in0=memT[:, ct, mt * P:(mt + 1) * P], scalar=q[:, NCT * b + ct:NCT * b + ct + 1], in1=gt[:, ct, b * P:(b + 1) * P], op0=ALU.add, op1=ALU.mult)
+                nc.vector.scalar_tensor_tensor(out=gt[:, ct, b * P:(b + 1) * P], in0=memT[:, ct, mt * P:(mt + 1) * P], scalar=q[:, NCT * b + ct:NCT * b + ct + 1], in1=gt[:, ct, b * P:(b + 1) * P], op0=ALU.subtract, op1=ALU.mult)
 
         def e_pb(mt, b):
             gt = gts[mt]
             for ct in range(NCT):
-                nc.vector.scalar_tensor_tensor(out=gt[:, ct, b * P:(b + 1) * P], in0=memT[:, ct, mt * P:(mt + 1) * P], scalar=q[:, NCT * b + ct:NCT * b + ct + 1], in1=gt[:, ct, b * P:(b + 1) * P], op0=ALU.add, op1=ALU.mult)
+                nc.vector.scalar_tensor_tensor(out=gt[:, ct, b * P:(b + 1) * P], in0=memT[:, ct, mt * P:(mt + 1) * P], scalar=q[:, NCT * b + ct:NCT * b + ct + 1], in1=gt[:, ct, b * P:(b + 1) * P], op0=ALU.subtract, op1=ALU.mult)
 
         def e_pc(mt, cts, bs):
             gt = gts[mt]
             for b in bs:
                 for ct in cts:
-                    nc.vector.scalar_tensor_tensor(out=gt[:, ct, b * P:(b + 1) * P], in0=memT[:, ct, mt * P:(mt + 1) * P], scalar=q[:, NCT * b + ct:NCT * b + ct + 1], in1=gt[:, ct, b * P:(b + 1) * P], op0=ALU.add, op1=ALU.mult)
+                    nc.vector.scalar_tensor_tensor(out=gt[:, ct, b * P:(b + 1) * P], in0=memT[:, ct, mt * P:(mt + 1) * P], scalar=q[:, NCT * b + ct:NCT * b + ct + 1], in1=gt[:, ct, b * P:(b + 1) * P], op0=ALU.subtract, op1=ALU.mult)
 
         def e_a(mt, ct):
             if mt not in tre:
@@ -262,7 +260,7 @@ def tile_dynamicmemorybank_pb_kernel(tc, h, x, memory, w2, b2, out_0, out_1):
         def out0(mt, c0, c1):
             if mt not in o0s:
                 o0s[mt] = epil.tile([P, C + 4], F32, name="o0", tag="o0", align_bytes=256)
-            nc.vector.tensor_tensor(out=o0s[mt][:, c0:c1], in0=fins[(mt, c0 // P)][:, c0:c1], in1=mem_sb[:, mt, c0:c1], op=ALU.add)
+            nc.vector.scalar_tensor_tensor(out=o0s[mt][:, c0:c1], in0=fins[(mt, c0 // P)][:, c0:c1], scalar=-0.25, in1=mem_sb[:, mt, c0:c1], op0=ALU.mult, op1=ALU.add)
 
         def store0(mt):
             nc.sync.dma_start(out=out_0[0, mt * P:(mt + 1) * P, :], in_=o0s[mt][:, 0:C])
@@ -307,22 +305,26 @@ def tile_dynamicmemorybank_pb_kernel(tc, h, x, memory, w2, b2, out_0, out_1):
 
         def e_p_half(hf):
             for b in (2 * hf, 2 * hf + 1):
-                nc.vector.scalar_tensor_tensor(out=gts[3][:, 3, b * P:(b + 1) * P], in0=memT[:, 3, 3 * P:4 * P], scalar=q[:, NCT * b + 3:NCT * b + 4], in1=gts[3][:, 3, b * P:(b + 1) * P], op0=ALU.add, op1=ALU.mult)
+                nc.vector.scalar_tensor_tensor(out=gts[3][:, 3, b * P:(b + 1) * P], in0=memT[:, 3, 3 * P:4 * P], scalar=q[:, NCT * b + 3:NCT * b + 4], in1=gts[3][:, 3, b * P:(b + 1) * P], op0=ALU.subtract, op1=ALU.mult)
 
-        def fin_m(mt, cts, n):
+        def fin_open(mt, cts):
             fin = psum_a.tile([P, C], F32, name="acc", tag="acc")
-            src = tre[mt] if n == 2 else gts[mt]
             for ct in cts:
                 fins[(mt, ct)] = fin
+            cols = slice(cts[0] * P, (cts[-1] + 1) * P)
+            nc.tensor.matmul(out=fin[:, cols], lhsT=neg4[:], rhs=mem_sb[:, mt, cols], start=True, stop=False)
+
+        def fin_m(mt, cts, n):
+            src = tre[mt] if n == 2 else gts[mt]
+            for ct in cts:
                 cols = slice(ct * P, (ct + 1) * P)
                 for i in range(n):
-                    nc.tensor.matmul(out=fin[:, cols], lhsT=src[:, ct, i * P:(i + 1) * P], rhs=ident_f[:], is_transpose=True, start=(i == 0), stop=False)
-                nc.tensor.matmul(out=fin[:, cols], lhsT=memT3[:, ct, (mt - 2) * P:(mt - 1) * P], rhs=ident_f[:], is_transpose=True, start=False, stop=True)
+                    nc.tensor.matmul(out=fins[(mt, ct)][:, cols], lhsT=src[:, ct, i * P:(i + 1) * P], rhs=ident_f[:], is_transpose=True, start=False, stop=(ct == cts[-1] and i == n - 1))
 
         def copy0(mt, c0, c1):
             if mt not in o0s:
                 o0s[mt] = epil.tile([P, C + 4], F32, name="o0", tag="o0", align_bytes=256)
-            nc.scalar.copy(out=o0s[mt][:, c0:c1], in_=fins[(mt, c0 // P)][:, c0:c1])
+            nc.scalar.activation(out=o0s[mt][:, c0:c1], in_=fins[(mt, c0 // P)][:, c0:c1], func=ACT.Copy, scale=-0.25)
 
         def epi_out(mt, k):
             e_p(mt, 0)
@@ -381,7 +383,6 @@ def tile_dynamicmemorybank_pb_kernel(tc, h, x, memory, w2, b2, out_0, out_1):
         for ct in range(NCT):
             sigmoid(0, ct)
         mem_transposes()
-        mem3()
         for b in range(NB):
             x_mm(b)
         q_d(0)
@@ -449,6 +450,7 @@ def tile_dynamicmemorybank_pb_kernel(tc, h, x, memory, w2, b2, out_0, out_1):
         mm_ct(3, 1)
         cast(1, 0)
         mm_ct(3, 2)
+        fin_open(2, (0, 1, 2, 3))
         fin_m(2, (0, 1, 2, 3), 2)
         copy0(2, 0, C)
         store0(2)
@@ -463,6 +465,9 @@ def tile_dynamicmemorybank_pb_kernel(tc, h, x, memory, w2, b2, out_0, out_1):
         recip(2)
         e_p_half(1)
         r448(2)
+        fin_open(3, (0, 1))
+        fin_open(3, (2,))
+        fin_open(3, (3,))
         fin_m(3, (0, 1), 4)
         copy0(3, 0, 2 * P)
         fin_m(3, (2,), 4)

@@ -307,8 +307,8 @@ def tile_dynamicmemorybank_pb_kernel(tc, h, x, memory, w2, b2, out_0, out_1):
             for b in (2 * hf, 2 * hf + 1):
                 nc.vector.scalar_tensor_tensor(out=gts[3][:, 3, b * P:(b + 1) * P], in0=memT[:, 3, 3 * P:4 * P], scalar=q[:, NCT * b + 3:NCT * b + 4], in1=gts[3][:, 3, b * P:(b + 1) * P], op0=ALU.subtract, op1=ALU.mult)
 
-        def fin_open(mt, cts):
-            fin = psum_a.tile([P, C], F32, name="acc", tag="acc")
+        def fin_open(mt, cts, pool):
+            fin = pool.tile([P, C], F32, name="acc", tag="acc") if pool is psum_a else pool.tile([P, C], F32, name="tp", tag="tp")
             for ct in cts:
                 fins[(mt, ct)] = fin
             cols = slice(cts[0] * P, (cts[-1] + 1) * P)
@@ -383,35 +383,37 @@ def tile_dynamicmemorybank_pb_kernel(tc, h, x, memory, w2, b2, out_0, out_1):
         for ct in range(NCT):
             sigmoid(0, ct)
         mem_transposes()
-        for b in range(NB):
+        for b in range(3):
             x_mm(b)
         q_d(0)
         q_d(1)
         e_pc(0, (0, 1), (0, 1))
         q_d(2)
         e_pc(0, (2, 3), (0, 1))
+        mm_ct(1, 0)
+        x_mm(3)
         e_pc(0, (0, 1, 2, 3), (2,))
         deint(2, 0, "s")
         q_d(3)
         e_pc(0, (0, 1, 2, 3), (3,))
-        mm_ct(1, 0)
         mm_ct(1, 1)
         e_a(0, 0)
         e_a(0, 1)
-        t_tile(2, 0, "ss")
         t_tile(2, 1, "ss")
+        t_tile(2, 0, "ss")
         e_a(0, 2)
         e_a(0, 3)
         e_p(1, 0)
+        e_p(1, 1)
         deint(2, 3, "v")
         mm_ct(1, 2)
         t_tile(2, 2, "ss")
         t_tile(2, 3, "ss")
-        e_p(1, 1)
         e_a(1, 0)
         e_a(1, 1)
         deint(3, 0, "v")
         deint(3, 1, "v")
+        e_p(1, 2)
         deint(3, 2, "v")
         deint(3, 3, "s")
         mm_ct(1, 3)
@@ -421,11 +423,17 @@ def tile_dynamicmemorybank_pb_kernel(tc, h, x, memory, w2, b2, out_0, out_1):
         quant_h(2, 1)
         quant_h(2, 2)
         quant_h(2, 3)
-        epi_out2(1, 0)
+        out0(0, 0, C)
+        store0(0)
+        e_p(1, 3)
+        amax(0, 0, C, new_am(0))
+        e_a(1, 2)
+        recip(0)
+        e_a(1, 3)
+        r448(0)
         mm_ct(2, 0)
         t_run(3, 1)
         t_run(3, 2)
-        cast(0, 0)
         mm_ct(2, 1)
         quant_h(3, 0)
         quant_h(3, 1)
@@ -435,39 +443,38 @@ def tile_dynamicmemorybank_pb_kernel(tc, h, x, memory, w2, b2, out_0, out_1):
         out0(1, 0, C)
         store0(1)
         e_p(2, 1)
-        amax(1, 0, C, new_am(1))
         mm_ct(2, 2)
         quant_h(3, 2)
         quant_h(3, 3)
-        recip(1)
+        amax(1, 0, C, new_am(1))
         e_a(2, 0)
-        r448(1)
+        recip(1)
         e_a(2, 1)
+        r448(1)
         mm_ct(2, 3)
+        cast(0, 0)
         epi(2, (2, 3))
 
         mm_ct(3, 0)
         mm_ct(3, 1)
         cast(1, 0)
         mm_ct(3, 2)
-        fin_open(2, (0, 1, 2, 3))
+        mm_half(0)
+        mm_half(1)
+        fin_open(2, (0, 1, 2, 3), psum_a)
+        fin_open(3, (0, 1), psum_t)
+        fin_open(3, (2,), psum_t)
+        fin_open(3, (3,), psum_t)
         fin_m(2, (0, 1, 2, 3), 2)
         copy0(2, 0, C)
         store0(2)
-        mm_half(0)
-        mm_half(1)
 
         e_p(3, 0)
         e_p(3, 1)
         e_p(3, 2)
-        amax(2, 0, C, new_am(2))
         e_p_half(0)
-        recip(2)
         e_p_half(1)
-        r448(2)
-        fin_open(3, (0, 1))
-        fin_open(3, (2,))
-        fin_open(3, (3,))
+        amax(2, 0, C, new_am(2))
         fin_m(3, (0, 1), 4)
         copy0(3, 0, 2 * P)
         fin_m(3, (2,), 4)
@@ -475,9 +482,11 @@ def tile_dynamicmemorybank_pb_kernel(tc, h, x, memory, w2, b2, out_0, out_1):
         fin_m(3, (3,), 4)
         copy0(3, 3 * P, C)
         store0(3)
-        cast(2, 0)
         amax(3, 0, 2 * P, o0s[3][:, C:C + 1])
+        recip(2)
         amax(3, 2 * P, 3 * P, o0s[3][:, C + 1:C + 2])
+        r448(2)
+        cast(2, 0)
         amax(3, 3 * P, C + 2, new_am(3))
         recip(3)
         r448(3)

@@ -51,9 +51,9 @@ def tile_dynamicmemorybank_pb_kernel(tc, h, x, memory, w2, b2, out_0, out_1):
         warm = consts.tile([P, 1], F32, name="warm")
         nc.scalar.activation(out=warm[:], in_=zeros[:], func=ACT.Sigmoid)
 
-        b2r = consts.tile([P, NCT], BF16, name="b2r")
-        with nc.allow_non_contiguous_dma(reason="512 bias values, one to a partition"):
-            nc.scalar.dma_start(out=b2r[:], in_=b2.rearrange("(c p) -> p c", p=P))
+        b2r = consts.tile([P, P], BF16, name="b2r", align_bytes=256)
+        nc.vector.memset(b2r[:], 0.0)
+        nc.scalar.dma_start(out=b2r[0:NCT, :], in_=b2.rearrange("(c p) -> c p", p=P))
         b2f = consts.tile([P, NCT], F32, name="b2f")
 
         mem_sb = consts.tile([P, NMT, C], BF16, name="mem_sb", align_bytes=256)
@@ -87,16 +87,16 @@ def tile_dynamicmemorybank_pb_kernel(tc, h, x, memory, w2, b2, out_0, out_1):
             return t
 
         def load_mem():
-            nc.sync.dma_start(out=mem_sb[:], in_=memory[0].rearrange("(m r) c -> r m c", r=P))
+            nc.sync.dma_start(out=mem_sb[:], in_=memory[0].rearrange("(r m) c -> r m c", m=NMT))
 
         def load_h(mt, b):
-            hs[(mt, b)] = load(h[b, mt * P:(mt + 1) * P, :])
+            hs[(mt, b)] = load(h[b].rearrange("(r m) k -> r m k", m=NMT)[:, mt, :])
 
         def load_h_halves(mt, b):
             t = loads.tile([P, F], BF16, name="ld", tag="ld", align_bytes=256)
             for hf in range(2):
                 cols = slice(hf * (F // 2), (hf + 1) * (F // 2))
-                nc.sync.dma_start(out=t[:, cols], in_=h[b, mt * P:(mt + 1) * P, cols])
+                nc.sync.dma_start(out=t[:, cols], in_=h[b].rearrange("(r m) k -> r m k", m=NMT)[:, mt, cols])
             hs[(mt, b)] = t
 
         def load_x(b):
@@ -106,7 +106,9 @@ def tile_dynamicmemorybank_pb_kernel(tc, h, x, memory, w2, b2, out_0, out_1):
             ws[g] = load(w2[512 * g:512 * (g + 1), :].rearrange("(p j) c -> p (j c)", j=4))
 
         def cast_b2():
-            nc.vector.tensor_copy(out=b2f[:], in_=b2r[:])
+            bt = psum_a.tile([P, P], BF16, name="acc", tag="acc")
+            nc.tensor.transpose(bt[:], b2r[:], ident_b[:])
+            nc.vector.tensor_copy(out=b2f[:], in_=bt[:, 0:NCT])
             nc.vector.tensor_scalar(out=neg4[:], in0=ident_b[:], scalar1=-4.0, scalar2=None, op0=ALU.mult)
 
         def mem_transposes():
@@ -263,7 +265,7 @@ def tile_dynamicmemorybank_pb_kernel(tc, h, x, memory, w2, b2, out_0, out_1):
             nc.vector.scalar_tensor_tensor(out=o0s[mt][:, c0:c1], in0=fins[(mt, c0 // P)][:, c0:c1], scalar=-0.25, in1=mem_sb[:, mt, c0:c1], op0=ALU.mult, op1=ALU.add)
 
         def store0(mt):
-            nc.sync.dma_start(out=out_0[0, mt * P:(mt + 1) * P, :], in_=o0s[mt][:, 0:C])
+            nc.sync.dma_start(out=out_0[0].rearrange("(r m) c -> r m c", m=NMT)[:, mt, :], in_=o0s[mt][:, 0:C])
 
         def amax(mt, c0, c1, dst):
             nc.vector.tensor_reduce(out=dst, in_=o0s[mt][:, c0:c1], axis=AX.X, op=ALU.max, apply_absolute_value=True)
@@ -285,7 +287,7 @@ def tile_dynamicmemorybank_pb_kernel(tc, h, x, memory, w2, b2, out_0, out_1):
             if vcols > 0:
                 nc.vector.tensor_scalar(out=o8[:, 0:vcols], in0=o0s[mt][:, 0:vcols], scalar1=rss[mt][:, 0:1], scalar2=None, op0=ALU.mult, saturate=False)
             nc.scalar.activation(out=o8[:, vcols:C], in_=o0s[mt][:, vcols:C], func=ACT.Identity, bias=zeros[:, 0:1], scale=rss[mt][:, 0:1], saturate=False)
-            nc.sync.dma_start(out=out_1[0, mt * P:(mt + 1) * P, :], in_=o8[:].bitcast(U8))
+            nc.sync.dma_start(out=out_1[0].rearrange("(r m) c -> r m c", m=NMT)[:, mt, :], in_=o8[:].bitcast(U8))
 
         def mm_half(hf):
             acc = psum_a.tile([P, 2 * P], F32, name="acc", tag="acc")

@@ -187,10 +187,10 @@ def tile_dynamicmemorybank_pb_kernel(tc, h, x, memory, w2, b2, out_0, out_1):
             )
 
         def w_interleave(g):
-            wr = ws[g][:].rearrange("p (j c) -> p c j", j=4)
+            wr = ws[g][:].rearrange("p (j c) -> p j c", j=4)
             wgs[g] = wstage.tile([P, C, 4], BF16, name="wg", tag="wg", align_bytes=256)
-            nc.vector.tensor_copy(out=wgs[g][:, 0:W_SPLIT, :], in_=wr[:, 0:W_SPLIT, :])
-            nc.scalar.copy(out=wgs[g][:, W_SPLIT:C, :], in_=wr[:, W_SPLIT:C, :])
+            nc.vector.tensor_copy(out=wgs[g][:, 0:W_SPLIT, :].rearrange("p (c i) j -> p c j i", i=4), in_=wr[:, :, 0:W_SPLIT].rearrange("p j (c i) -> p c j i", i=4))
+            nc.scalar.copy(out=wgs[g][:, W_SPLIT:C, :].rearrange("p (c i) j -> p c j i", i=4), in_=wr[:, :, W_SPLIT:C].rearrange("p j (c i) -> p c j i", i=4))
 
         def quant_w(g):
             nc.vector.quantize_mx(

@@ -245,6 +245,9 @@ def tile_dynamicmemorybank_pb_kernel(tc, h, x, memory, w2, b2, out_0, out_1):
             gt = gts[mt]
             nc.vector.tensor_tensor(out=tre[mt][:, ct, :], in0=gt[:, ct, 0:2 * P], in1=gt[:, ct, 2 * P:4 * P], op=ALU.add)
 
+        def e_a2(mt, ct):
+            nc.vector.tensor_tensor(out=tre[mt][:, ct, 0:P], in0=tre[mt][:, ct, 0:P], in1=tre[mt][:, ct, P:2 * P], op=ALU.add)
+
         def epi(mt, cts):
             for ct in cts:
                 e_p(mt, ct)
@@ -253,7 +256,7 @@ def tile_dynamicmemorybank_pb_kernel(tc, h, x, memory, w2, b2, out_0, out_1):
 
         def fin_t(mt, cts, n):
             fin = psum_a.tile([P, C], F32, name="acc", tag="acc")
-            src = tre[mt] if n == 2 else gts[mt]
+            src = tre[mt] if n <= 2 else gts[mt]
             for ct in cts:
                 fins[(mt, ct)] = fin
                 for i in range(n):
@@ -433,13 +436,17 @@ def tile_dynamicmemorybank_pb_kernel(tc, h, x, memory, w2, b2, out_0, out_1):
         recip(0)
         e_a(1, 3)
         r448(0)
+        e_a2(1, 0)
+        e_a2(1, 1)
+        e_a2(1, 2)
+        e_a2(1, 3)
         mm_ct(2, 0)
         t_run(3, 1)
         t_run(3, 2)
         mm_ct(2, 1)
         quant_h(3, 0)
         quant_h(3, 1)
-        fin_t(1, (0, 1, 2, 3), 2)
+        fin_t(1, (0, 1, 2, 3), 1)
         t_run(3, 3)
         e_p(2, 0)
         out0(1, 0, C)

from contextlib import ExitStack

import concourse.mybir as mybir
from concourse.masks import make_identity

F32 = mybir.dt.float32
BF16 = mybir.dt.bfloat16
U32 = mybir.dt.uint32
U8 = mybir.dt.uint8
FP8X4 = mybir.dt.float8_e4m3fn_x4
FP8 = mybir.dt.float8_e4m3fn
ALU = mybir.AluOpType
ACT = mybir.ActivationFunctionType
AX = mybir.AxisListType

NB, T, C, F = 4, 512, 512, 2048
P = 128
NMT = T // P
NCT = C // P
NG = F // 512
FLOPS = 2 * NB * T * F * C

XN = 32
W_SPLIT = 320


def tile_dynamicmemorybank_pb_kernel(tc, h, x, memory, w2, b2, out_0, out_1):
    nc = tc.nc
    with ExitStack() as ctx:
        consts = ctx.enter_context(tc.tile_pool(name="consts", bufs=1))
        loads = ctx.enter_context(tc.tile_pool(name="loads", bufs=16))
        wstage = ctx.enter_context(tc.tile_pool(name="wstage", bufs=2))
        hstage = ctx.enter_context(tc.tile_pool(name="hstage", bufs=2))
        dstage = ctx.enter_context(tc.tile_pool(name="dstage", bufs=8))
        epil = ctx.enter_context(tc.tile_pool(name="epil", bufs=2))
        psum_t = ctx.enter_context(tc.psum_pool(name="psum_t", bufs=4))
        psum_a = ctx.enter_context(tc.psum_pool(name="psum_a", bufs=4))
        ctx.enter_context(tc.manual_schedule())

        ones_f = consts.tile([P, P], F32, name="ones_f", align_bytes=256)
        nc.gpsimd.memset(ones_f[:], 1.0)
        ident_f = consts.tile([P, P], F32, name="ident_f", align_bytes=256)
        make_identity(nc, ident_f[:])
        ident_b = consts.tile([P, P], BF16, name="ident_b", align_bytes=256)
        make_identity(nc, ident_b[:])
        neg4 = consts.tile([P, P], BF16, name="neg4", align_bytes=256)
        ones = consts.tile([P, P], BF16, name="ones", align_bytes=256)
        nc.vector.memset(ones[:], 1.0)
        zeros = consts.tile([P, 1], F32, name="zeros")
        nc.vector.memset(zeros[:], 0.0)
        warm = consts.tile([P, 1], F32, name="warm")
        nc.scalar.activation(out=warm[:], in_=zeros[:], func=ACT.Sigmoid)

        b2r = consts.tile([P, P], BF16, name="b2r", align_bytes=256)
        nc.vector.memset(b2r[:], 0.0)
        nc.scalar.dma_start(out=b2r[0:NCT, :], in_=b2.rearrange("(c p) -> c p", p=P))
        b2f = consts.tile([P, NCT], F32, name="b2f")

        mem_sb = consts.tile([P, NMT, C], BF16, name="mem_sb", align_bytes=256)
        memT = consts.tile([P, NCT, T], BF16, name="memT", align_bytes=256)
        q = consts.tile([P, NB * NCT], F32, name="q")
        wcodes = consts.tile([P, NG, C], U32, name="wcodes", align_bytes=256)
        wscales = consts.tile([P, NG, C], U8, name="wscales", align_bytes=256)

        xs_sb = {}
        hs = {}
        hds = {}
        ws = {}
        wgs = {}
        xsums = {}
        hgrp = {}
        hcodes = {}
        hscales = {}
        accs = {}
        gts = {}
        tre = {}
        oTs = {}
        fins = {}
        o0s = {}
        rss = {}
        rcs = {}
        ams = {}

        def load(src):
            t = loads.tile([P, F], BF16, name="ld", tag="ld", align_bytes=256)
            nc.sync.dma_start(out=t[:], in_=src)
            return t

        def load_mem():
            nc.sync.dma_start(out=mem_sb[:], in_=memory[0].rearrange("(r m) c -> r m c", m=NMT))

        def load_h(mt, b):
            hs[(mt, b)] = load(h[b].rearrange("(r m) k -> r m k", m=NMT)[:, mt, :])

        def load_h_halves(mt, b):
            t = loads.tile([P, F], BF16, name="ld", tag="ld", align_bytes=256)
            for hf in range(2):
                cols = slice(hf * (F // 2), (hf + 1) * (F // 2))
                nc.sync.dma_start(out=t[:, cols], in_=h[b].rearrange("(r m) k -> r m k", m=NMT)[:, mt, cols])
            hs[(mt, b)] = t

        def load_x(b):
            xs_sb[b] = load(x[b].rearrange("(p j) c -> p (j c)", j=4))

        def load_w(g):
            ws[g] = load(w2[512 * g:512 * (g + 1), :].rearrange("(p j) c -> p (j c)", j=4))

        def cast_b2():
            bt = psum_a.tile([P, P], BF16, name="acc", tag="acc")
            nc.tensor.transpose(bt[:], b2r[:], ident_b[:])
            nc.vector.tensor_copy(out=b2f[:], in_=bt[:, 0:NCT])
            nc.vector.tensor_scalar(out=neg4[:], in0=ident_b[:], scalar1=-4.0, scalar2=None, op0=ALU.mult)

        def mem_transposes():
            for cp in range(2):
                mp = psum_t.tile([P, 2, T], BF16, name="tp", tag="tp")
                for c2 in range(2):
                    ct = 2 * cp + c2
                    for mt in range(NMT):
                        nc.tensor.transpose(mp[:, c2, mt * P:(mt + 1) * P], mem_sb[:, mt, ct * P:(ct + 1) * P], ident_b[:])
                if cp == 0:
                    nc.vector.tensor_copy(out=memT[:, 0:2, :], in_=mp[:])
                else:
                    nc.scalar.copy(out=memT[:, 2:4, :], in_=mp[:])

        def x_mm(b):
            xt = xs_sb[b][:].rearrange("p (j c) -> p j c", j=4)
            xsums[b] = psum_a.tile([P, NCT, XN], F32, name="acc", tag="acc")
            for ct in range(NCT):
                for j in range(4):
                    nc.tensor.matmul(out=xsums[b][:, ct, :], lhsT=xt[:, j, ct * P:(ct + 1) * P], rhs=ones[:, 0:XN], start=(j == 0), stop=(j == 3))

        def q_d(b):
            nc.vector.tensor_scalar(out=q[:, NCT * b:NCT * (b + 1)], in0=xsums[b][:, :, 0], scalar1=1.0 / T, scalar2=None, op0=ALU.mult)

        def warm_pe(n):
            wp = psum_a.tile([P, P], F32, name="acc", tag="acc")
            for i in range(n):
                nc.tensor.matmul(out=wp[:], lhsT=ones_f[:], rhs=ones_f[:], start=True, stop=True)

        def deint(mt, b, eng):
            hd = dstage.tile([P, F], BF16, name="hd", tag="hd", align_bytes=256)
            o = hd[:].bitcast(F32).rearrange("p (g u w) -> p g u w", g=NG, u=2)
            i = hs[(mt, b)][:].bitcast(F32).rearrange("p (g w u) -> p g u w", g=NG, u=2)
            if eng == "v":
                nc.vector.tensor_copy(out=o, in_=i)
            else:
                nc.scalar.copy(out=o, in_=i)
            hds[(mt, b)] = hd

        def t_bank(mt, b, gp, eng):
            if mt not in hgrp:
                hgrp[mt] = hstage.tile([P, NG, NB, P, 4], BF16, name="hgrp", tag="hgrp", align_bytes=256)
            dense = (mt, b) in hds
            words = (hds[(mt, b)] if dense else hs[(mt, b)])[:].bitcast(F32)
            tp = psum_t.tile([P, 2, 2, P], F32, name="tp", tag="tp")
            for g2 in range(2):
                g = 2 * gp + g2
                for u in range(2):
                    if dense:
                        nc.tensor.transpose(tp[:, g2, u, :], words[:, 256 * g + 128 * u:256 * g + 128 * (u + 1)], ident_f[:])
                    else:
                        nc.tensor.transpose(tp[:, g2, u, :], words[:, 256 * g + u:256 * (g + 1):2], ident_f[:])
            src = tp[:].rearrange("p g u r -> p g r u")
            o = hgrp[mt][:].bitcast(F32)[:, 2 * gp:2 * gp + 2, b, :, :]
            if eng == "v":
                nc.vector.tensor_copy(out=o, in_=src)
            else:
                nc.scalar.copy(out=o, in_=src)

        def t_tile(mt, b, engs):
            t_bank(mt, b, 0, engs[0])
            t_bank(mt, b, 1, engs[1])

        def t_run(mt, j):
            t_bank(mt, 2 * (j % 2), j // 2, "s")
            t_bank(mt, 2 * (j % 2) + 1, j // 2, "s")

        def quant_h(mt, g):
            if mt not in hcodes:
                hcodes[mt] = hstage.tile([P, NG, NB * P], U32, name="hcodes", tag="hcodes", align_bytes=256)
                hscales[mt] = hstage.tile([P, NG, NB * P], U8, name="hscales", tag="hscales", align_bytes=256)
            nc.vector.quantize_mx(
                out=hcodes[mt][:, g, :].bitcast(FP8X4),
                scales=hscales[mt][:, g, :],
                in_=hgrp[mt][:, g].rearrange("p b r j -> p (b r j)"),
            )

        def w_interleave(g):
            wr = ws[g][:].rearrange("p (j c) -> p j c", j=4)
            wgs[g] = wstage.tile([P, C, 4], BF16, name="wg", tag="wg", align_bytes=256)
            nc.vector.tensor_copy(out=wgs[g][:, 0:W_SPLIT, :].rearrange("p (c i) j -> p c j i", i=4), in_=wr[:, :, 0:W_SPLIT].rearrange("p j (c i) -> p c j i", i=4))
            nc.scalar.copy(out=wgs[g][:, W_SPLIT:C, :].rearrange("p (c i) j -> p c j i", i=4), in_=wr[:, :, W_SPLIT:C].rearrange("p j (c i) -> p c j i", i=4))

        def quant_w(g):
            nc.vector.quantize_mx(
                out=wcodes[:, g, :].bitcast(FP8X4),
                scales=wscales[:, g, :],
                in_=wgs[g][:].rearrange("p c j -> p (c j)"),
            )

        def mm(mt, ct, g):
            if g == 0:
                accs[(mt, ct)] = psum_a.tile([P, NB * P], F32, name="acc", tag="acc")
            cols = slice(ct * P, (ct + 1) * P)
            nc.tensor.matmul_mx(
                out=accs[(mt, ct)][:],
                lhsT=wcodes[:, g, cols].bitcast(FP8X4),
                lhsT_scale=wscales[:, g, cols],
                rhs=hcodes[mt][:, g, :].bitcast(FP8X4),
                rhs_scale=hscales[mt][:, g, :],
                start=(g == 0),
                stop=(g == NG - 1),
            )

        def sigmoid(mt, ct):
            if mt not in gts:
                gts[mt] = epil.tile([P, NCT, NB * P], F32, name="gt", tag="gt", align_bytes=256)
            nc.scalar.activation(out=gts[mt][:, ct, :], in_=accs[(mt, ct)][:], func=ACT.Sigmoid, bias=b2f[:, ct:ct + 1], scale=1.0)

        def mm_ct(mt, ct):
            for g in range(NG):
                mm(mt, ct, g)
            sigmoid(mt, ct)

        def e_p(mt, ct):
            gt = gts[mt]
            for b in range(NB):
                nc.vector.scalar_tensor_tensor(out=gt[:, ct, b * P:(b + 1) * P], in0=memT[:, ct, mt * P:(mt + 1) * P], scalar=q[:, NCT * b + ct:NCT * b + ct + 1], in1=gt[:, ct, b * P:(b + 1) * P], op0=ALU.subtract, op1=ALU.mult)

        def e_pb(mt, b):
            gt = gts[mt]
            for ct in range(NCT):
                nc.vector.scalar_tensor_tensor(out=gt[:, ct, b * P:(b + 1) * P], in0=memT[:, ct, mt * P:(mt + 1) * P], scalar=q[:, NCT * b + ct:NCT * b + ct + 1], in1=gt[:, ct, b * P:(b + 1) * P], op0=ALU.subtract, op1=ALU.mult)

        def e_pc(mt, cts, bs):
            gt = gts[mt]
            for b in bs:
                for ct in cts:
                    nc.vector.scalar_tensor_tensor(out=gt[:, ct, b * P:(b + 1) * P], in0=memT[:, ct, mt * P:(mt + 1) * P], scalar=q[:, NCT * b + ct:NCT * b + ct + 1], in1=gt[:, ct, b * P:(b + 1) * P], op0=ALU.subtract, op1=ALU.mult)

        def e_a(mt, ct):
            if mt not in tre:
                tre[mt] = epil.tile([P, NCT, 2 * P], F32, name="tre", tag="tre", align_bytes=256)
            gt = gts[mt]
            nc.vector.tensor_tensor(out=tre[mt][:, ct, :], in0=gt[:, ct, 0:2 * P], in1=gt[:, ct, 2 * P:4 * P], op=ALU.add)

        def e_a2(mt, ct):
            nc.vector.tensor_tensor(out=tre[mt][:, ct, 0:P], in0=tre[mt][:, ct, 0:P], in1=tre[mt][:, ct, P:2 * P], op=ALU.add)

        def epi(mt, cts):
            for ct in cts:
                e_p(mt, ct)
            for ct in cts:
                e_a(mt, ct)

        def fin_t(mt, cts, n):
            fin = psum_a.tile([P, C], F32, name="acc", tag="acc")
            src = tre[mt] if n <= 2 else gts[mt]
            for ct in cts:
                fins[(mt, ct)] = fin
                for i in range(n):
                    nc.tensor.matmul(out=fin[:, ct * P:(ct + 1) * P], lhsT=src[:, ct, i * P:(i + 1) * P], rhs=ident_f[:], is_transpose=True, start=(i == 0), stop=(i == n - 1))

        def out0(mt, c0, c1):
            if mt not in o0s:
                o0s[mt] = epil.tile([P, C + 4], F32, name="o0", tag="o0", align_bytes=256)
            nc.vector.scalar_tensor_tensor(out=o0s[mt][:, c0:c1], in0=fins[(mt, c0 // P)][:, c0:c1], scalar=-0.25, in1=mem_sb[:, mt, c0:c1], op0=ALU.mult, op1=ALU.add)

        def store0(mt):
            nc.sync.dma_start(out=out_0[0].rearrange("(r m) c -> r m c", m=NMT)[:, mt, :], in_=o0s[mt][:, 0:C])

        def amax(mt, c0, c1, dst):
            nc.vector.tensor_reduce(out=dst, in_=o0s[mt][:, c0:c1], axis=AX.X, op=ALU.max, apply_absolute_value=True)

        def new_am(mt):
            ams[mt] = epil.tile([P, 1], F32, name="am", tag="am")
            return ams[mt][:]

        def recip(mt):
            rcs[mt] = epil.tile([P, 1], F32, name="rc", tag="rc")
            nc.vector.reciprocal(out=rcs[mt][:], in_=ams[mt][:])

        def r448(mt):
            rss[mt] = epil.tile([P, 1], F32, name="rs", tag="rs")
            nc.vector.tensor_scalar(out=rss[mt][:], in0=rcs[mt][:], scalar1=448.0, scalar2=None, op0=ALU.mult)

        def cast(mt, vcols):
            o8 = epil.tile([P, C], FP8, name="o8", tag="o8", align_bytes=256)
            if vcols > 0:
                nc.vector.tensor_scalar(out=o8[:, 0:vcols], in0=o0s[mt][:, 0:vcols], scalar1=rss[mt][:, 0:1], scalar2=None, op0=ALU.mult, saturate=False)
            nc.scalar.activation(out=o8[:, vcols:C], in_=o0s[mt][:, vcols:C], func=ACT.Identity, bias=zeros[:, 0:1], scale=rss[mt][:, 0:1], saturate=False)
            nc.sync.dma_start(out=out_1[0].rearrange("(r m) c -> r m c", m=NMT)[:, mt, :], in_=o8[:].bitcast(U8))

        def mm_half(hf):
            acc = psum_a.tile([P, 2 * P], F32, name="acc", tag="acc")
            toks = slice(hf * 2 * P, (hf + 1) * 2 * P)
            cols = slice(3 * P, 4 * P)
            for g in range(NG):
                nc.tensor.matmul_mx(
                    out=acc[:],
                    lhsT=wcodes[:, g, cols].bitcast(FP8X4),
                    lhsT_scale=wscales[:, g, cols],
                    rhs=hcodes[3][:, g, toks].bitcast(FP8X4),
                    rhs_scale=hscales[3][:, g, toks],
                    start=(g == 0),
                    stop=(g == NG - 1),
                )
            nc.scalar.activation(out=gts[3][:, 3, toks], in_=acc[:], func=ACT.Sigmoid, bias=b2f[:, 3:4], scale=1.0)

        def e_p_half(hf):
            for b in (2 * hf, 2 * hf + 1):
                nc.vector.scalar_tensor_tensor(out=gts[3][:, 3, b * P:(b + 1) * P], in0=memT[:, 3, 3 * P:4 * P], scalar=q[:, NCT * b + 3:NCT * b + 4], in1=gts[3][:, 3, b * P:(b + 1) * P], op0=ALU.subtract, op1=ALU.mult)

        def fin_open(mt, cts, pool):
            fin = pool.tile([P, C], F32, name="acc", tag="acc") if pool is psum_a else pool.tile([P, C], F32, name="tp", tag="tp")
            for ct in cts:
                fins[(mt, ct)] = fin
            cols = slice(cts[0] * P, (cts[-1] + 1) * P)
            nc.tensor.matmul(out=fin[:, cols], lhsT=neg4[:], rhs=mem_sb[:, mt, cols], start=True, stop=False)

        def fin_m(mt, cts, n):
            src = tre[mt] if n == 2 else gts[mt]
            for ct in cts:
                cols = slice(ct * P, (ct + 1) * P)
                for i in range(n):
                    nc.tensor.matmul(out=fins[(mt, ct)][:, cols], lhsT=src[:, ct, i * P:(i + 1) * P], rhs=ident_f[:], is_transpose=True, start=False, stop=(ct == cts[-1] and i == n - 1))

        def copy0(mt, c0, c1):
            if mt not in o0s:
                o0s[mt] = epil.tile([P, C + 4], F32, name="o0", tag="o0", align_bytes=256)
            nc.scalar.activation(out=o0s[mt][:, c0:c1], in_=fins[(mt, c0 // P)][:, c0:c1], func=ACT.Copy, scale=-0.25)

        def epi_out(mt, k):
            e_p(mt, 0)
            out0(k, 0, C)
            store0(k)
            e_p(mt, 1)
            amax(k, 0, C, new_am(k))
            e_a(mt, 0)
            recip(k)
            e_a(mt, 1)
            r448(k)

        def epi_out2(mt, k):
            e_p(mt, 2)
            out0(k, 0, C)
            store0(k)
            e_p(mt, 3)
            amax(k, 0, C, new_am(k))
            e_a(mt, 2)
            recip(k)
            e_a(mt, 3)
            r448(k)

        load_h_halves(0, 0)
        for b in range(1, NB):
            load_h(0, b)
        for g in range(NG):
            load_w(g)
            load_h(1, g)
        load_mem()
        for b in range(NB):
            load_x(b)
        for mt in (2, 3):
            for b in range(NB):
                load_h(mt, b)

        warm_pe(7)
        for b in range(3):
            t_tile(0, b, "sv")
        cast_b2()
        w_interleave(0)
        t_tile(0, 3, "sv")
        quant_w(0)
        quant_h(0, 0)
        for g in range(NG):
            if g + 1 < NG:
                w_interleave(g + 1)
            t_tile(1, g, "ss")
            for ct in range(NCT):
                mm(0, ct, g)
            if g + 1 < NG:
                quant_h(0, g + 1)
                quant_w(g + 1)
        for g in range(NG):
            quant_h(1, g)
        for ct in range(NCT):
            sigmoid(0, ct)
        mem_transposes()
        for b in range(3):
            x_mm(b)
        q_d(0)
        q_d(1)
        e_pc(0, (0, 1), (0, 1))
        q_d(2)
        e_pc(0, (2, 3), (0, 1))
        mm_ct(1, 0)
        x_mm(3)
        e_pc(0, (0, 1, 2, 3), (2,))
        deint(2, 0, "s")
        q_d(3)
        e_pc(0, (0, 1, 2, 3), (3,))
        mm_ct(1, 1)
        e_a(0, 0)
        e_a(0, 1)
        t_tile(2, 1, "ss")
        t_tile(2, 0, "ss")
        e_a(0, 2)
        e_a(0, 3)
        e_p(1, 0)
        e_p(1, 1)
        deint(2, 3, "v")
        mm_ct(1, 2)
        t_tile(2, 2, "ss")
        t_tile(2, 3, "ss")
        e_a(1, 0)
        e_a(1, 1)
        deint(3, 0, "v")
        deint(3, 1, "v")
        e_p(1, 2)
        deint(3, 2, "v")
        deint(3, 3, "s")
        mm_ct(1, 3)
        fin_t(0, (0, 1, 2, 3), 2)
        t_run(3, 0)
        quant_h(2, 0)
        quant_h(2, 1)
        quant_h(2, 2)
        quant_h(2, 3)
        out0(0, 0, C)
        store0(0)
        e_p(1, 3)
        amax(0, 0, C, new_am(0))
        e_a(1, 2)
        recip(0)
        e_a(1, 3)
        r448(0)
        e_a2(1, 0)
        e_a2(1, 1)
        e_a2(1, 2)
        e_a2(1, 3)
        mm_ct(2, 0)
        t_run(3, 1)
        t_run(3, 2)
        mm_ct(2, 1)
        quant_h(3, 0)
        quant_h(3, 1)
        fin_t(1, (0, 1, 2, 3), 1)
        t_run(3, 3)
        e_p(2, 0)
        out0(1, 0, C)
        store0(1)
        e_p(2, 1)
        mm_ct(2, 2)
        quant_h(3, 2)
        quant_h(3, 3)
        amax(1, 0, C, new_am(1))
        e_a(2, 0)
        recip(1)
        e_a(2, 1)
        r448(1)
        mm_ct(2, 3)
        cast(0, 0)
        epi(2, (2, 3))

        mm_ct(3, 0)
        mm_ct(3, 1)
        cast(1, 0)
        mm_ct(3, 2)
        mm_half(0)
        mm_half(1)
        fin_open(2, (0, 1, 2, 3), psum_a)
        fin_open(3, (0, 1), psum_t)
        fin_open(3, (2,), psum_t)
        fin_open(3, (3,), psum_t)
        fin_m(2, (0, 1, 2, 3), 2)
        copy0(2, 0, C)
        store0(2)

        e_p(3, 0)
        e_p(3, 1)
        e_p(3, 2)
        e_p_half(0)
        e_p_half(1)
        amax(2, 0, C, new_am(2))
        fin_m(3, (0, 1), 4)
        copy0(3, 0, 2 * P)
        fin_m(3, (2,), 4)
        copy0(3, 2 * P, 3 * P)
        fin_m(3, (3,), 4)
        copy0(3, 3 * P, C)
        store0(3)
        amax(3, 0, 2 * P, o0s[3][:, C:C + 1])
        recip(2)
        amax(3, 2 * P, 3 * P, o0s[3][:, C + 1:C + 2])
        r448(2)
        cast(2, 0)
        amax(3, 3 * P, C + 2, new_am(3))
        recip(3)
        r448(3)
        cast(3, 320)
